import numpy as np
import ml_dtypes


def mxq(x, axis, fmt="e4m3"):
    dtype, down = {"e4m3": (ml_dtypes.float8_e4m3fn, 7), "e5m2": (ml_dtypes.float8_e5m2, 14)}[fmt]
    v = np.moveaxis(np.asarray(x, np.float32).astype(ml_dtypes.bfloat16).astype(np.float64), axis, -1)
    blocks = v.reshape(v.shape[:-1] + (-1, 32))
    amax = np.abs(blocks).max(-1, keepdims=True)
    byte = np.maximum(np.where(amax > 0, np.frexp(amax)[1] - 1 + 127, 0) - down, 1)
    scale = np.exp2(byte - 127.0)
    codes = (blocks / scale).astype(np.float32).astype(dtype).astype(np.float64)
    return np.moveaxis((codes * scale).reshape(v.shape), -1, axis)


WIDE = False


def mx_kscale(k):
    if not WIDE:
        return np.ones(k)
    levels = np.array([10, -10, 5, -5, 0])
    if k % 512:
        return np.exp2(np.random.permutation(np.resize(levels, k // 32))).repeat(32)
    a = np.empty((k // 512, 16))
    for p in range(k // 512):
        a[p, :8] = np.random.permutation(np.resize(levels, 8))
        for g in range(8):
            far = levels[np.abs(levels - a[p, g]) >= 10]
            a[p, g + 8] = far[np.random.randint(len(far))]
    return np.exp2(a.ravel()).repeat(32)


BF16 = ml_dtypes.bfloat16


def bf(x):
    return np.asarray(x, np.float32).astype(BF16)


def f64(x):
    return np.asarray(x).astype(np.float64)


B, S, D, QR, KR, H, NOPE, ROPE, VD = 2, 64, 1024, 1536, 512, 16, 64, 64, 64
EPS = 1e-6
THETA = 10000.0
LAT = 3.0 * np.sqrt(EPS)


def rmsnorm(x, w):
    var = np.mean(x * x, axis=-1, keepdims=True)
    return w * (x * (1.0 / np.sqrt(var + EPS)))


def rope_cos_sin(seq_len):
    inv_freq = 1.0 / (THETA ** (f64(np.arange(0, ROPE, 2)) / ROPE))
    t = f64(np.arange(seq_len))
    freqs = np.outer(t, inv_freq)
    emb = np.concatenate([freqs, freqs], -1)
    return np.cos(emb), np.sin(emb)


def rotate_half(x):
    x1, x2 = x[..., : x.shape[-1] // 2], x[..., x.shape[-1] // 2 :]
    return np.concatenate([-x2, x1], axis=-1)


def setup_inputs():
    s, t = mx_kscale(D), mx_kscale(KR)
    return {"hidden_states": bf(np.random.standard_normal((B, S, D)) * s),
            "kv_a_w_ckv": bf(np.random.standard_normal((KR, D)) * LAT / np.sqrt(D) / s[None, :]),
            "k_pe_raw": bf(np.random.standard_normal((B, S, ROPE))),
            "kv_a_ln_w": bf((1.0 + 0.1 * np.random.standard_normal(KR)) * t),
            "kv_b_w": bf(np.random.standard_normal((H * (NOPE + VD), KR)) / np.sqrt(KR) / t[None, :])}


def reference(hidden_states, kv_a_w_ckv, k_pe_raw, kv_a_ln_w, kv_b_w):
    ckv = mxq(f64(hidden_states), 2, "e4m3") @ mxq(f64(kv_a_w_ckv), 1, "e4m3").T
    ckv_n = rmsnorm(ckv, f64(kv_a_ln_w))
    kv = mxq(ckv_n, 2, "e4m3") @ mxq(f64(kv_b_w), 1, "e4m3").T
    kv = kv.reshape(B, S, H, NOPE + VD).transpose(0, 2, 1, 3)
    k_nope, v = kv[..., :NOPE], kv[..., NOPE:]
    k_pe = f64(k_pe_raw).reshape(B, 1, S, ROPE)
    cos, sin = rope_cos_sin(S)
    cos, sin = cos[None, None], sin[None, None]
    k_pe = k_pe * cos + rotate_half(k_pe) * sin
    key_s = np.concatenate([k_nope, np.broadcast_to(k_pe, (B, H, S, ROPE))], -1)
    return key_s, v

@@ -1,0 +1,305 @@
+import math
+from contextlib import ExitStack
+
+import concourse.mybir as mybir
+from concourse.masks import make_identity
+
+F32 = mybir.dt.float32
+BF16 = mybir.dt.bfloat16
+U32 = mybir.dt.uint32
+U8 = mybir.dt.uint8
+I32 = mybir.dt.int32
+FP8X4 = mybir.dt.float8_e4m3fn_x4
+ACT = mybir.ActivationFunctionType
+ALU = mybir.AluOpType
+
+P = 128
+PACK = 4
+BATCH, SEQ = 2, 64
+TOK = BATCH * SEQ
+D = 1024
+KR = 512
+HEADS, HEAD_COLS, HALF_HEAD = 16, 128, 64
+ROPE, ROPE_HALF = 64, 32
+PASSES_1 = D // (P * PACK)
+CHUNKS = KR // P
+QUARTERS = 4
+QUARTER_ROWS = HEADS * HEAD_COLS // QUARTERS
+HEADS_PER_QUARTER = HEADS // QUARTERS
+EPS = 1e-6
+THETA = 10000.0
+ROUND_MAGIC = 12582912.0
+
+FLOPS = 2 * TOK * D * KR + 2 * TOK * KR * HEADS * HEAD_COLS
+
+
+def transpose_words(nc, bank, rows_bf16, ident):
+    words = rows_bf16.bitcast(F32)
+    for u in range(2):
+        nc.tensor.transpose(bank[:, u, :], words[:, u::2], ident)
+
+
+def tile_modelnew_pb_s_kernel(
+    tc, hidden_states, kv_a_w_ckv, k_pe_raw, kv_a_ln_w, kv_b_w, key_s, v
+):
+    nc = tc.nc
+    with ExitStack() as ctx:
+        keep = ctx.enter_context(tc.tile_pool(name="keep", bufs=1))
+        staging = ctx.enter_context(tc.psum_pool(name="staging", bufs=3))
+        products = ctx.enter_context(tc.psum_pool(name="products", bufs=4))
+        norm_psum = ctx.enter_context(tc.psum_pool(name="norm_psum", bufs=1))
+        ctx.enter_context(tc.manual_schedule())
+
+        x_sb = keep.tile([P, D], BF16)
+        nc.sync.dma_start(out=x_sb[:], in_=hidden_states.flatten_outer_dims())
+        wa_sb = keep.tile([P, CHUNKS, D], BF16)
+        wa_rows = kv_a_w_ckv.rearrange("(p t) k -> t p k", t=CHUNKS)
+        for t in range(CHUNKS):
+            nc.sync.dma_start(out=wa_sb[:, t, :], in_=wa_rows[t])
+        wb_sb = keep.tile([P, QUARTERS, PACK, KR], BF16)
+        wb_rows = kv_b_w.rearrange("(q p i) k -> q p i k", q=QUARTERS, i=PACK)
+        for q in range(QUARTERS):
+            nc.sync.dma_start(out=wb_sb[:, q], in_=wb_rows[q])
+        pe_sb = keep.tile([P, ROPE], BF16)
+        for b in range(BATCH):
+            nc.scalar.dma_start(out=pe_sb[b:P:BATCH, :], in_=k_pe_raw[b])
+        gain_bf = keep.tile([P, CHUNKS], BF16)
+        nc.scalar.dma_start(out=gain_bf[:], in_=kv_a_ln_w.rearrange("(p t) -> p t", t=CHUNKS))
+
+        partition_no = keep.tile([P, 1], I32)
+        nc.gpsimd.iota(partition_no[:], pattern=[[0, 1]], base=0, channel_multiplier=1)
+        ident = keep.tile([P, P], F32)
+        make_identity(nc, ident[:])
+        ones = keep.tile([P, P], F32)
+        nc.vector.memset(ones[:], 1.0)
+
+        freq = keep.tile([P, 2, ROPE_HALF], F32)
+        nc.vector.memset(freq[:, :, 0:1], 1.0)
+        for step in range(5):
+            w = 2**step
+            nc.vector.tensor_scalar(
+                out=freq[:, :, w : 2 * w],
+                in0=freq[:, :, 0:w],
+                scalar1=THETA ** (-w / ROPE_HALF),
+                scalar2=None,
+                op0=ALU.mult,
+            )
+        eps = keep.tile([P, 1], F32)
+        nc.vector.tensor_scalar(
+            out=eps[:], in0=freq[:, 0, 0:1], scalar1=EPS, scalar2=None, op0=ALU.mult
+        )
+        pos_int = keep.tile([P, 1], I32)
+        nc.vector.tensor_single_scalar(
+            out=pos_int[:], in_=partition_no[:], scalar=1, op=ALU.arith_shift_right
+        )
+        pos = keep.tile([P, 1], F32)
+        nc.vector.tensor_copy(out=pos[:], in_=pos_int[:])
+        turns = keep.tile([P, 2, ROPE_HALF], F32)
+        nc.vector.tensor_scalar(
+            out=turns[:],
+            in0=freq[:],
+            scalar1=pos[:, 0:1],
+            scalar2=1.0 / (2.0 * math.pi),
+            op0=ALU.mult,
+            op1=ALU.mult,
+        )
+        nc.vector.tensor_scalar_add(out=turns[:, 1, :], in0=turns[:, 1, :], scalar1=0.25)
+        whole = keep.tile([P, 2, ROPE_HALF], F32)
+        nc.vector.tensor_scalar(
+            out=whole[:],
+            in0=turns[:],
+            scalar1=ROUND_MAGIC,
+            scalar2=ROUND_MAGIC,
+            op0=ALU.add,
+            op1=ALU.subtract,
+        )
+        frac = keep.tile([P, 2, ROPE_HALF], F32)
+        nc.vector.tensor_tensor(out=frac[:], in0=turns[:], in1=whole[:], op=ALU.subtract)
+        sin_cos = keep.tile([P, 2, ROPE_HALF], F32)
+        nc.scalar.activation(out=sin_cos[:], in_=frac[:], func=ACT.Sin, scale=2.0 * math.pi)
+        table_warm = keep.tile([P, 1], F32)
+        nc.scalar.activation(out=table_warm[:], in_=sin_cos[:, 1, 0:1], func=ACT.Abs_reciprocal_sqrt)
+
+        gain = keep.tile([P, CHUNKS], F32)
+        nc.gpsimd.tensor_copy(out=gain[:], in_=gain_bf[:])
+        prod = keep.tile([P, 2, 2, ROPE_HALF], F32)
+        nc.gpsimd.tensor_tensor(
+            out=prod[:],
+            in0=pe_sb[:].rearrange("p (h j) -> p h j", h=2).unsqueeze(1).to_broadcast([P, 2, 2, ROPE_HALF]),
+            in1=sin_cos[:].unsqueeze(2).to_broadcast([P, 2, 2, ROPE_HALF]),
+            op=ALU.mult,
+        )
+        rope = keep.tile([P, ROPE], F32)
+        nc.gpsimd.tensor_tensor(
+            out=rope[:, 0:ROPE_HALF], in0=prod[:, 1, 0, :], in1=prod[:, 0, 1, :], op=ALU.subtract
+        )
+        nc.gpsimd.tensor_tensor(
+            out=rope[:, ROPE_HALF:ROPE], in0=prod[:, 1, 1, :], in1=prod[:, 0, 0, :], op=ALU.add
+        )
+        for b in range(BATCH):
+            nc.sync.dma_start(
+                out=key_s[b].rearrange("h s d -> s h d")[:, :, HALF_HEAD:HEAD_COLS],
+                in_=rope[b:P:BATCH, :].unsqueeze(1).to_broadcast([SEQ, HEADS, ROPE]),
+            )
+
+        x_grouped = keep.tile([P, PASSES_1, TOK, PACK], BF16, align_bytes=64)
+        x_codes = keep.tile([P, PASSES_1, TOK], U32, align_bytes=64)
+        x_scales = keep.tile([P, PASSES_1, TOK], U8, align_bytes=64)
+        x_bank = staging.tile([P, PASSES_1, 2, TOK], F32, tag="bank")
+        for g in range(PASSES_1):
+            transpose_words(nc, x_bank[:, g], x_sb[:, KR * g : KR * (g + 1)], ident[:])
+        for g in range(PASSES_1):
+            nc.vector.tensor_copy(
+                out=x_grouped[:, g].bitcast(F32).rearrange("p (s b) u -> p s b u", b=BATCH),
+                in_=x_bank[:, g].rearrange("p u (b s) -> p s b u", b=BATCH),
+            )
+
+        wa_grouped = keep.tile([P, CHUNKS, PASSES_1, P, PACK], BF16, align_bytes=64)
+        wa_codes = keep.tile([P, CHUNKS, PASSES_1, P], U32, align_bytes=64)
+        wa_scales = keep.tile([P, CHUNKS, PASSES_1, P], U8, align_bytes=64)
+        for t in range(CHUNKS):
+            wa_bank = staging.tile([P, PASSES_1, 2, P], F32, tag="bank")
+            for g in range(PASSES_1):
+                transpose_words(nc, wa_bank[:, g], wa_sb[:, t, KR * g : KR * (g + 1)], ident[:])
+            copy_out = nc.vector.tensor_copy if t == 0 else nc.scalar.copy
+            copy_out(
+                out=wa_grouped[:, t].bitcast(F32), in_=wa_bank[:].rearrange("p g u m -> p g m u")
+            )
+            if t == 0:
+                nc.vector.quantize_mx(
+                    out=x_codes[:].rearrange("p g r -> p (g r)").bitcast(FP8X4),
+                    scales=x_scales[:].rearrange("p g r -> p (g r)"),
+                    in_=x_grouped[:].rearrange("p g r k -> p (g r k)"),
+                )
+            nc.vector.quantize_mx(
+                out=wa_codes[:, t].rearrange("p g m -> p (g m)").bitcast(FP8X4),
+                scales=wa_scales[:, t].rearrange("p g m -> p (g m)"),
+                in_=wa_grouped[:, t].rearrange("p g m k -> p (g m k)"),
+            )
+
+        wb_grouped = keep.tile([P, QUARTERS, 2, 2 * P, PACK], BF16, align_bytes=64)
+        wb_codes = keep.tile([P, QUARTERS, QUARTER_ROWS], U32, align_bytes=64)
+        wb_scales = keep.tile([P, QUARTERS, QUARTER_ROWS], U8, align_bytes=64)
+
+        def transpose_and_regroup_wb(q, half):
+            wb_bank = staging.tile([P, 2, 2, P], F32, tag="bank")
+            for j in range(2):
+                transpose_words(nc, wb_bank[:, j], wb_sb[:, q, 2 * half + j, :], ident[:])
+            copy_out = nc.vector.tensor_copy if q == 0 else nc.scalar.copy
+            copy_out(
+                out=wb_grouped[:, q, half].bitcast(F32).rearrange("p (j n) u -> p j n u", j=2),
+                in_=wb_bank[:].rearrange("p j u n -> p j n u"),
+            )
+
+        def quantise_wb(q, half):
+            cols = slice(2 * P * half, 2 * P * (half + 1))
+            nc.vector.quantize_mx(
+                out=wb_codes[:, q, cols].bitcast(FP8X4),
+                scales=wb_scales[:, q, cols],
+                in_=wb_grouped[:, q, half].rearrange("p c k -> p (c k)"),
+            )
+
+        squares = keep.tile([P, CHUNKS, TOK], F32)
+        gained = keep.tile([P, CHUNKS, TOK], F32)
+
+        def first_product(t):
+            ckv_t = products.tile([P, TOK], F32, tag="product")
+            for g in range(PASSES_1):
+                nc.tensor.matmul_mx(
+                    out=ckv_t[:],
+                    lhsT=wa_codes[:, t, g, :].bitcast(FP8X4),
+                    lhsT_scale=wa_scales[:, t, g, :],
+                    rhs=x_codes[:, g, :].bitcast(FP8X4),
+                    rhs_scale=x_scales[:, g, :],
+                    start=(g == 0),
+                    stop=(g == PASSES_1 - 1),
+                )
+            nc.scalar.activation(out=squares[:, t, :], in_=ckv_t[:], func=ACT.Square)
+            nc.vector.tensor_scalar(
+                out=gained[:, t, :], in0=ckv_t[:], scalar1=gain[:, t : t + 1], scalar2=None, op0=ALU.mult
+            )
+
+        first_product(0)
+        first_product(1)
+        squares_01 = keep.tile([P, TOK], F32)
+        nc.vector.tensor_tensor(
+            out=squares_01[:], in0=squares[:, 0, :], in1=squares[:, 1, :], op=ALU.add
+        )
+        first_product(2)
+        squares_012 = keep.tile([P, TOK], F32)
+        nc.vector.tensor_tensor(
+            out=squares_012[:], in0=squares_01[:], in1=squares[:, 2, :], op=ALU.add
+        )
+        transpose_and_regroup_wb(0, 0)
+        first_product(CHUNKS - 1)
+        quantise_wb(0, 0)
+        transpose_and_regroup_wb(0, 1)
+
+        sum_sq = norm_psum.tile([P, TOK], F32)
+        nc.tensor.matmul(out=sum_sq[:], lhsT=ones[:], rhs=squares_012[:], start=True, stop=False)
+        nc.tensor.matmul(
+            out=sum_sq[:], lhsT=ones[:], rhs=squares[:, CHUNKS - 1, :], start=False, stop=True
+        )
+        rstd = keep.tile([P, TOK], F32)
+        nc.scalar.activation(
+            out=rstd[:], in_=sum_sq[:], func=ACT.Abs_reciprocal_sqrt, bias=eps[:, 0:1], scale=1.0 / KR
+        )
+        quantise_wb(0, 1)
+        transpose_and_regroup_wb(1, 0)
+        cn_grouped = keep.tile([P, TOK, PACK], BF16, align_bytes=64)
+        nc.vector.tensor_tensor(
+            out=cn_grouped[:],
+            in0=gained[:].rearrange("p t r -> p r t"),
+            in1=rstd[:].unsqueeze(2).to_broadcast([P, TOK, PACK]),
+            op=ALU.mult,
+        )
+        cn_codes = keep.tile([P, TOK], U32, align_bytes=64)
+        cn_scales = keep.tile([P, TOK], U8, align_bytes=64)
+        nc.vector.quantize_mx(
+            out=cn_codes[:].bitcast(FP8X4),
+            scales=cn_scales[:],
+            in_=cn_grouped[:].rearrange("p r k -> p (r k)"),
+        )
+        quantise_wb(1, 0)
+
+        kv_sb = keep.tile([P, HEADS * HEAD_COLS], F32)
+
+        def second_product(q):
+            kv_ps = products.tile([P, QUARTER_ROWS], F32, tag="product")
+            nc.tensor.matmul_mx(
+                out=kv_ps[:],
+                lhsT=cn_codes[:].bitcast(FP8X4),
+                lhsT_scale=cn_scales[:],
+                rhs=wb_codes[:, q, :].bitcast(FP8X4),
+                rhs_scale=wb_scales[:, q, :],
+                start=True,
+                stop=True,
+            )
+            kv_cols = slice(QUARTER_ROWS * q, QUARTER_ROWS * (q + 1))
+            nc.vector.tensor_copy(
+                out=kv_sb[:, kv_cols].rearrange("p (n i) -> p n i", i=PACK),
+                in_=kv_ps[:].rearrange("p (i n) -> p n i", i=PACK),
+            )
+            heads = slice(HEADS_PER_QUARTER * q, HEADS_PER_QUARTER * (q + 1))
+            for b in range(BATCH):
+                by_head = kv_sb[b:P:BATCH, kv_cols].rearrange("s (h c) -> s h c", c=HEAD_COLS)
+                nc.sync.dma_start(
+                    out=key_s[b, heads, :, 0:HALF_HEAD].rearrange("h s d -> s h d"),
+                    in_=by_head[:, :, 0:HALF_HEAD],
+                )
+                nc.sync.dma_start(
+                    out=v[b, heads].rearrange("h s d -> s h d"),
+                    in_=by_head[:, :, HALF_HEAD:HEAD_COLS],
+                )
+
+        transpose_and_regroup_wb(1, 1)
+        quantise_wb(1, 1)
+        for half in range(2):
+            transpose_and_regroup_wb(2, half)
+            quantise_wb(2, half)
+        second_product(0)
+        for half in range(2):
+            transpose_and_regroup_wb(3, half)
+            quantise_wb(3, half)
+            second_product(1 + half)
+        second_product(3)

@@ -23,9 +23,9 @@ HEADS, HEAD_COLS, HALF_HEAD = 16, 128, 64
 ROPE, ROPE_HALF = 64, 32
 PASSES_1 = D // (P * PACK)
 CHUNKS = KR // P
-QUARTERS = 4
-QUARTER_ROWS = HEADS * HEAD_COLS // QUARTERS
-HEADS_PER_QUARTER = HEADS // QUARTERS
+PARTS = 8
+PART_ROWS = HEADS * HEAD_COLS // PARTS
+HEADS_PER_QUARTER = 4
 EPS = 1e-6
 THETA = 10000.0
 ROUND_MAGIC = 12582912.0
@@ -45,8 +45,8 @@ def tile_modelnew_pb_s_kernel(
     nc = tc.nc
     with ExitStack() as ctx:
         keep = ctx.enter_context(tc.tile_pool(name="keep", bufs=1))
-        staging = ctx.enter_context(tc.psum_pool(name="staging", bufs=3))
-        products = ctx.enter_context(tc.psum_pool(name="products", bufs=4))
+        staging = ctx.enter_context(tc.psum_pool(name="staging", bufs=4))
+        products = ctx.enter_context(tc.psum_pool(name="products", bufs=3))
         norm_psum = ctx.enter_context(tc.psum_pool(name="norm_psum", bufs=1))
         ctx.enter_context(tc.manual_schedule())
 
@@ -56,15 +56,17 @@ def tile_modelnew_pb_s_kernel(
         wa_rows = kv_a_w_ckv.rearrange("(p t) k -> t p k", t=CHUNKS)
         for t in range(CHUNKS):
             nc.sync.dma_start(out=wa_sb[:, t, :], in_=wa_rows[t])
-        wb_sb = keep.tile([P, QUARTERS, PACK, KR], BF16)
-        wb_rows = kv_b_w.rearrange("(q p i) k -> q p i k", q=QUARTERS, i=PACK)
-        for q in range(QUARTERS):
-            nc.sync.dma_start(out=wb_sb[:, q], in_=wb_rows[q])
         pe_sb = keep.tile([P, ROPE], BF16)
         for b in range(BATCH):
-            nc.scalar.dma_start(out=pe_sb[b:P:BATCH, :], in_=k_pe_raw[b])
+            nc.sync.dma_start(out=pe_sb[b:P:BATCH, :], in_=k_pe_raw[b])
         gain_bf = keep.tile([P, CHUNKS], BF16)
-        nc.scalar.dma_start(out=gain_bf[:], in_=kv_a_ln_w.rearrange("(p t) -> p t", t=CHUNKS))
+        nc.sync.dma_start(out=gain_bf[:], in_=kv_a_ln_w.rearrange("(p t) -> p t", t=CHUNKS))
+        wb_sb = keep.tile([P, PARTS, 2, KR], BF16)
+        wb_rows = kv_b_w.rearrange("(m p i) k -> p m (i k)", m=PARTS, i=2)
+        for m in range(0, PARTS, 2):
+            nc.sync.dma_start(
+                out=wb_sb[:, m : m + 2].rearrange("p m i k -> p m (i k)"), in_=wb_rows[:, m : m + 2]
+            )
 
         partition_no = keep.tile([P, 1], I32)
         nc.gpsimd.iota(partition_no[:], pattern=[[0, 1]], base=0, channel_multiplier=1)
@@ -73,37 +75,42 @@ def tile_modelnew_pb_s_kernel(
         ones = keep.tile([P, P], F32)
         nc.vector.memset(ones[:], 1.0)
 
-        freq = keep.tile([P, 2, ROPE_HALF], F32)
-        nc.vector.memset(freq[:, :, 0:1], 1.0)
-        for step in range(5):
-            w = 2**step
+        turn_rate = keep.tile([P, ROPE_HALF], F32)
+        for j in range(PACK):
             nc.vector.tensor_scalar(
-                out=freq[:, :, w : 2 * w],
-                in0=freq[:, :, 0:w],
-                scalar1=THETA ** (-w / ROPE_HALF),
+                out=turn_rate[:, j : j + 1],
+                in0=ones[:, 0:1],
+                scalar1=THETA ** (-j / ROPE_HALF) / (2.0 * math.pi),
                 scalar2=None,
                 op0=ALU.mult,
             )
-        eps = keep.tile([P, 1], F32)
-        nc.vector.tensor_scalar(
-            out=eps[:], in0=freq[:, 0, 0:1], scalar1=EPS, scalar2=None, op0=ALU.mult
-        )
         pos_int = keep.tile([P, 1], I32)
         nc.vector.tensor_single_scalar(
             out=pos_int[:], in_=partition_no[:], scalar=1, op=ALU.arith_shift_right
         )
-        pos = keep.tile([P, 1], F32)
-        nc.vector.tensor_copy(out=pos[:], in_=pos_int[:])
+        eps = keep.tile([P, 1], F32)
+        nc.vector.tensor_scalar(out=eps[:], in0=ones[:, 0:1], scalar1=EPS, scalar2=None, op0=ALU.mult)
+        for j in range(PACK, ROPE_HALF, PACK):
+            nc.vector.tensor_scalar(
+                out=turn_rate[:, j : j + PACK],
+                in0=turn_rate[:, 0:PACK],
+                scalar1=THETA ** (-j / ROPE_HALF),
+                scalar2=None,
+                op0=ALU.mult,
+            )
+            if j == PACK:
+                pos = keep.tile([P, 1], F32)
+                nc.vector.tensor_copy(out=pos[:], in_=pos_int[:])
         turns = keep.tile([P, 2, ROPE_HALF], F32)
-        nc.vector.tensor_scalar(
-            out=turns[:],
-            in0=freq[:],
-            scalar1=pos[:, 0:1],
-            scalar2=1.0 / (2.0 * math.pi),
-            op0=ALU.mult,
-            op1=ALU.mult,
-        )
-        nc.vector.tensor_scalar_add(out=turns[:, 1, :], in0=turns[:, 1, :], scalar1=0.25)
+        for i, quarter in enumerate((0.0, 0.25)):
+            nc.vector.tensor_scalar(
+                out=turns[:, i, :],
+                in0=turn_rate[:],
+                scalar1=pos[:, 0:1],
+                scalar2=quarter,
+                op0=ALU.mult,
+                op1=ALU.add,
+            )
         whole = keep.tile([P, 2, ROPE_HALF], F32)
         nc.vector.tensor_scalar(
             out=whole[:],
@@ -120,8 +127,6 @@ def tile_modelnew_pb_s_kernel(
         table_warm = keep.tile([P, 1], F32)
         nc.scalar.activation(out=table_warm[:], in_=sin_cos[:, 1, 0:1], func=ACT.Abs_reciprocal_sqrt)
 
-        gain = keep.tile([P, CHUNKS], F32)
-        nc.gpsimd.tensor_copy(out=gain[:], in_=gain_bf[:])
         prod = keep.tile([P, 2, 2, ROPE_HALF], F32)
         nc.gpsimd.tensor_tensor(
             out=prod[:],
@@ -141,10 +146,127 @@ def tile_modelnew_pb_s_kernel(
                 out=key_s[b].rearrange("h s d -> s h d")[:, :, HALF_HEAD:HEAD_COLS],
                 in_=rope[b:P:BATCH, :].unsqueeze(1).to_broadcast([SEQ, HEADS, ROPE]),
             )
+        gain = keep.tile([P, CHUNKS], F32)
+        nc.gpsimd.tensor_copy(out=gain[:], in_=gain_bf[:])
 
         x_grouped = keep.tile([P, PASSES_1, TOK, PACK], BF16, align_bytes=64)
         x_codes = keep.tile([P, PASSES_1, TOK], U32, align_bytes=64)
         x_scales = keep.tile([P, PASSES_1, TOK], U8, align_bytes=64)
+        wa_grouped = keep.tile([P, CHUNKS, PASSES_1, P, PACK], BF16, align_bytes=64)
+        wa_codes = keep.tile([P, CHUNKS, PASSES_1, P], U32, align_bytes=64)
+        wa_scales = keep.tile([P, CHUNKS, PASSES_1, P], U8, align_bytes=64)
+        wb_grouped = keep.tile([P, PARTS, PART_ROWS, PACK], BF16, align_bytes=64)
+        wb_codes = keep.tile([P, PARTS * PART_ROWS], U32, align_bytes=64)
+        wb_scales = keep.tile([P, PARTS * PART_ROWS], U8, align_bytes=64)
+        squares = keep.tile([P, CHUNKS, TOK], F32)
+        gained = keep.tile([P, CHUNKS, TOK], F32)
+        kv_sb = [keep.tile([P, 2 * PART_ROWS], F32, name=f"kv_sb_{q}") for q in range(PARTS // 2)]
+        banks = {}
+        sum_sq = norm_psum.tile([P, TOK], F32)
+
+        def transpose_wa(t):
+            bank = staging.tile([P, PASSES_1, 2, P], F32, tag="bank")
+            for g in range(PASSES_1):
+                transpose_words(nc, bank[:, g], wa_sb[:, t, KR * g : KR * (g + 1)], ident[:])
+            banks["a", t] = bank
+
+        def regroup_wa(copy_out, t):
+            copy_out(
+                out=wa_grouped[:, t].bitcast(F32),
+                in_=banks["a", t][:].rearrange("p g u m -> p g m u"),
+            )
+
+        def quantise_wa(t):
+            nc.vector.quantize_mx(
+                out=wa_codes[:, t].rearrange("p g m -> p (g m)").bitcast(FP8X4),
+                scales=wa_scales[:, t].rearrange("p g m -> p (g m)"),
+                in_=wa_grouped[:, t].rearrange("p g m k -> p (g m k)"),
+            )
+
+        def transpose_wb(m, rows=(0, 1)):
+            if 0 in rows:
+                banks["b", m] = staging.tile([P, 2, 2, P], F32, tag="bank", name="wb_bank")
+            for i in rows:
+                transpose_words(nc, banks["b", m][:, i], wb_sb[:, m, i, :], ident[:])
+
+        def regroup_wb(copy_out, m):
+            copy_out(
+                out=wb_grouped[:, m].bitcast(F32).rearrange("p (i n) u -> p i n u", i=2),
+                in_=banks["b", m][:].rearrange("p i u n -> p i n u"),
+            )
+
+        def quantise_wb(m):
+            cols = slice(PART_ROWS * m, PART_ROWS * (m + 1))
+            nc.vector.quantize_mx(
+                out=wb_codes[:, cols].bitcast(FP8X4),
+                scales=wb_scales[:, cols],
+                in_=wb_grouped[:, m].rearrange("p c k -> p (c k)"),
+            )
+
+        ckv_01 = products.tile([P, 2, TOK], F32, tag="product")
+        ckv_23 = products.tile([P, 2, TOK], F32, tag="product")
+        ckv = [ckv_01, ckv_23]
+
+        def first_product(t):
+            for g in range(PASSES_1):
+                nc.tensor.matmul_mx(
+                    out=ckv[t // 2][:, t % 2, :],
+                    lhsT=wa_codes[:, t, g, :].bitcast(FP8X4),
+                    lhsT_scale=wa_scales[:, t, g, :],
+                    rhs=x_codes[:, g, :].bitcast(FP8X4),
+                    rhs_scale=x_scales[:, g, :],
+                    start=(g == 0),
+                    stop=(g == PASSES_1 - 1),
+                )
+
+        def multiply_by_gain(pair):
+            chunks = slice(2 * pair, 2 * pair + 2)
+            nc.vector.tensor_tensor(
+                out=gained[:, chunks, :],
+                in0=ckv[pair][:],
+                in1=gain[:, chunks].unsqueeze(2).to_broadcast([P, 2, TOK]),
+                op=ALU.mult,
+            )
+
+        def add_over_partitions(values, start=False, stop=False):
+            nc.tensor.matmul(out=sum_sq[:], lhsT=ones[:], rhs=values, start=start, stop=stop)
+
+        def second_product(parts):
+            cols = slice(PART_ROWS * parts[0], PART_ROWS * (parts[-1] + 1))
+            kv_ps = products.tile([P, PART_ROWS * len(parts)], F32, tag="product")
+            nc.tensor.matmul_mx(
+                out=kv_ps[:],
+                lhsT=cn_codes[:].bitcast(FP8X4),
+                lhsT_scale=cn_scales[:],
+                rhs=wb_codes[:, cols].bitcast(FP8X4),
+                rhs_scale=wb_scales[:, cols],
+                start=True,
+                stop=True,
+            )
+            banks["kv", parts] = kv_ps
+
+        def copy_kv(copy_out, parts):
+            q, lo = parts[0] // 2, PART_ROWS * (parts[0] % 2)
+            copy_out(
+                out=kv_sb[q][:, lo : lo + PART_ROWS * len(parts)].rearrange(
+                    "p (h n i) -> p h n i", n=P, i=2
+                ),
+                in_=banks["kv", parts][:].rearrange("p (h i n) -> p h n i", n=P, i=2),
+            )
+
+        def store_kv(q, b, queue):
+            heads = slice(HEADS_PER_QUARTER * q, HEADS_PER_QUARTER * (q + 1))
+            by_head = kv_sb[q][b:P:BATCH, :].rearrange("s (h c) -> s h c", c=HEAD_COLS)
+            queue.dma_start(
+                out=key_s[b, heads, :, 0:HALF_HEAD].rearrange("h s d -> s h d"),
+                in_=by_head[:, :, 0:HALF_HEAD],
+            )
+            queue.dma_start(
+                out=v[b, heads].rearrange("h s d -> s h d"), in_=by_head[:, :, HALF_HEAD:HEAD_COLS]
+            )
+
+        on_vector, on_scalar = nc.vector.tensor_copy, nc.scalar.copy
+
         x_bank = staging.tile([P, PASSES_1, 2, TOK], F32, tag="bank")
         for g in range(PASSES_1):
             transpose_words(nc, x_bank[:, g], x_sb[:, KR * g : KR * (g + 1)], ident[:])
@@ -153,99 +275,54 @@ def tile_modelnew_pb_s_kernel(
                 out=x_grouped[:, g].bitcast(F32).rearrange("p (s b) u -> p s b u", b=BATCH),
                 in_=x_bank[:, g].rearrange("p u (b s) -> p s b u", b=BATCH),
             )
-
-        wa_grouped = keep.tile([P, CHUNKS, PASSES_1, P, PACK], BF16, align_bytes=64)
-        wa_codes = keep.tile([P, CHUNKS, PASSES_1, P], U32, align_bytes=64)
-        wa_scales = keep.tile([P, CHUNKS, PASSES_1, P], U8, align_bytes=64)
-        for t in range(CHUNKS):
-            wa_bank = staging.tile([P, PASSES_1, 2, P], F32, tag="bank")
-            for g in range(PASSES_1):
-                transpose_words(nc, wa_bank[:, g], wa_sb[:, t, KR * g : KR * (g + 1)], ident[:])
-            copy_out = nc.vector.tensor_copy if t == 0 else nc.scalar.copy
-            copy_out(
-                out=wa_grouped[:, t].bitcast(F32), in_=wa_bank[:].rearrange("p g u m -> p g m u")
-            )
-            if t == 0:
-                nc.vector.quantize_mx(
-                    out=x_codes[:].rearrange("p g r -> p (g r)").bitcast(FP8X4),
-                    scales=x_scales[:].rearrange("p g r -> p (g r)"),
-                    in_=x_grouped[:].rearrange("p g r k -> p (g r k)"),
-                )
-            nc.vector.quantize_mx(
-                out=wa_codes[:, t].rearrange("p g m -> p (g m)").bitcast(FP8X4),
-                scales=wa_scales[:, t].rearrange("p g m -> p (g m)"),
-                in_=wa_grouped[:, t].rearrange("p g m k -> p (g m k)"),
-            )
-
-        wb_grouped = keep.tile([P, QUARTERS, 2, 2 * P, PACK], BF16, align_bytes=64)
-        wb_codes = keep.tile([P, QUARTERS, QUARTER_ROWS], U32, align_bytes=64)
-        wb_scales = keep.tile([P, QUARTERS, QUARTER_ROWS], U8, align_bytes=64)
-
-        def transpose_and_regroup_wb(q, half):
-            wb_bank = staging.tile([P, 2, 2, P], F32, tag="bank")
-            for j in range(2):
-                transpose_words(nc, wb_bank[:, j], wb_sb[:, q, 2 * half + j, :], ident[:])
-            copy_out = nc.vector.tensor_copy if q == 0 else nc.scalar.copy
-            copy_out(
-                out=wb_grouped[:, q, half].bitcast(F32).rearrange("p (j n) u -> p j n u", j=2),
-                in_=wb_bank[:].rearrange("p j u n -> p j n u"),
-            )
-
-        def quantise_wb(q, half):
-            cols = slice(2 * P * half, 2 * P * (half + 1))
-            nc.vector.quantize_mx(
-                out=wb_codes[:, q, cols].bitcast(FP8X4),
-                scales=wb_scales[:, q, cols],
-                in_=wb_grouped[:, q, half].rearrange("p c k -> p (c k)"),
-            )
-
-        squares = keep.tile([P, CHUNKS, TOK], F32)
-        gained = keep.tile([P, CHUNKS, TOK], F32)
-
-        def first_product(t):
-            ckv_t = products.tile([P, TOK], F32, tag="product")
-            for g in range(PASSES_1):
-                nc.tensor.matmul_mx(
-                    out=ckv_t[:],
-                    lhsT=wa_codes[:, t, g, :].bitcast(FP8X4),
-                    lhsT_scale=wa_scales[:, t, g, :],
-                    rhs=x_codes[:, g, :].bitcast(FP8X4),
-                    rhs_scale=x_scales[:, g, :],
-                    start=(g == 0),
-                    stop=(g == PASSES_1 - 1),
-                )
-            nc.scalar.activation(out=squares[:, t, :], in_=ckv_t[:], func=ACT.Square)
-            nc.vector.tensor_scalar(
-                out=gained[:, t, :], in0=ckv_t[:], scalar1=gain[:, t : t + 1], scalar2=None, op0=ALU.mult
-            )
+        nc.vector.quantize_mx(
+            out=x_codes[:].rearrange("p g r -> p (g r)").bitcast(FP8X4),
+            scales=x_scales[:].rearrange("p g r -> p (g r)"),
+            in_=x_grouped[:].rearrange("p g r k -> p (g r k)"),
+        )
+        transpose_wa(0)
+        regroup_wa(on_scalar, 0)
+        transpose_wa(1)
+        regroup_wa(on_vector, 1)
+        transpose_wa(2)
+        regroup_wa(on_scalar, 2)
+        transpose_wa(3)
+        quantise_wa(0)
+        quantise_wa(1)
+        regroup_wa(on_vector, 3)
+        quantise_wa(2)
+        quantise_wa(3)
 
         first_product(0)
         first_product(1)
+        nc.scalar.activation(out=squares[:, 0:2], in_=ckv[0][:], func=ACT.Square)
+        transpose_wb(0)
         squares_01 = keep.tile([P, TOK], F32)
         nc.vector.tensor_tensor(
             out=squares_01[:], in0=squares[:, 0, :], in1=squares[:, 1, :], op=ALU.add
         )
+        multiply_by_gain(0)
+        regroup_wb(on_scalar, 0)
+        transpose_wb(1)
         first_product(2)
-        squares_012 = keep.tile([P, TOK], F32)
-        nc.vector.tensor_tensor(
-            out=squares_012[:], in0=squares_01[:], in1=squares[:, 2, :], op=ALU.add
-        )
-        transpose_and_regroup_wb(0, 0)
-        first_product(CHUNKS - 1)
-        quantise_wb(0, 0)
-        transpose_and_regroup_wb(0, 1)
+        first_product(3)
+        nc.scalar.activation(out=squares[:, 2, :], in_=ckv[1][:, 0, :], func=ACT.Square)
+        nc.scalar.activation(out=squares[:, 3, :], in_=ckv[1][:, 1, :], func=ACT.Square)
+        quantise_wb(0)
+        multiply_by_gain(1)
+        regroup_wb(on_scalar, 1)
 
-        sum_sq = norm_psum.tile([P, TOK], F32)
-        nc.tensor.matmul(out=sum_sq[:], lhsT=ones[:], rhs=squares_012[:], start=True, stop=False)
-        nc.tensor.matmul(
-            out=sum_sq[:], lhsT=ones[:], rhs=squares[:, CHUNKS - 1, :], start=False, stop=True
-        )
+        add_over_partitions(squares_01[:], start=True)
+        transpose_wb(2, (0,))
+        add_over_partitions(squares[:, 2, :])
+        add_over_partitions(squares[:, 3, :], stop=True)
         rstd = keep.tile([P, TOK], F32)
         nc.scalar.activation(
             out=rstd[:], in_=sum_sq[:], func=ACT.Abs_reciprocal_sqrt, bias=eps[:, 0:1], scale=1.0 / KR
         )
-        quantise_wb(0, 1)
-        transpose_and_regroup_wb(1, 0)
+        transpose_wb(2, (1,))
+        regroup_wb(on_scalar, 2)
+        quantise_wb(1)
         cn_grouped = keep.tile([P, TOK, PACK], BF16, align_bytes=64)
         nc.vector.tensor_tensor(
             out=cn_grouped[:],
@@ -253,6 +330,7 @@ def tile_modelnew_pb_s_kernel(
             in1=rstd[:].unsqueeze(2).to_broadcast([P, TOK, PACK]),
             op=ALU.mult,
         )
+        quantise_wb(2)
         cn_codes = keep.tile([P, TOK], U32, align_bytes=64)
         cn_scales = keep.tile([P, TOK], U8, align_bytes=64)
         nc.vector.quantize_mx(
@@ -260,46 +338,37 @@ def tile_modelnew_pb_s_kernel(
             scales=cn_scales[:],
             in_=cn_grouped[:].rearrange("p r k -> p (r k)"),
         )
-        quantise_wb(1, 0)
+        transpose_wb(3)
+        regroup_wb(on_scalar, 3)
+        transpose_wb(4)
+        regroup_wb(on_vector, 4)
+        quantise_wb(3)
+        transpose_wb(5)
+        quantise_wb(4)
 
-        kv_sb = keep.tile([P, HEADS * HEAD_COLS], F32)
-
-        def second_product(q):
-            kv_ps = products.tile([P, QUARTER_ROWS], F32, tag="product")
-            nc.tensor.matmul_mx(
-                out=kv_ps[:],
-                lhsT=cn_codes[:].bitcast(FP8X4),
-                lhsT_scale=cn_scales[:],
-                rhs=wb_codes[:, q, :].bitcast(FP8X4),
-                rhs_scale=wb_scales[:, q, :],
-                start=True,
-                stop=True,
-            )
-            kv_cols = slice(QUARTER_ROWS * q, QUARTER_ROWS * (q + 1))
-            nc.vector.tensor_copy(
-                out=kv_sb[:, kv_cols].rearrange("p (n i) -> p n i", i=PACK),
-                in_=kv_ps[:].rearrange("p (i n) -> p n i", i=PACK),
-            )
-            heads = slice(HEADS_PER_QUARTER * q, HEADS_PER_QUARTER * (q + 1))
+        def store_quarter(q, queues):
             for b in range(BATCH):
-                by_head = kv_sb[b:P:BATCH, kv_cols].rearrange("s (h c) -> s h c", c=HEAD_COLS)
-                nc.sync.dma_start(
-                    out=key_s[b, heads, :, 0:HALF_HEAD].rearrange("h s d -> s h d"),
-                    in_=by_head[:, :, 0:HALF_HEAD],
-                )
-                nc.sync.dma_start(
-                    out=v[b, heads].rearrange("h s d -> s h d"),
-                    in_=by_head[:, :, HALF_HEAD:HEAD_COLS],
-                )
+                store_kv(q, b, queues[b])
 
-        transpose_and_regroup_wb(1, 1)
-        quantise_wb(1, 1)
-        for half in range(2):
-            transpose_and_regroup_wb(2, half)
-            quantise_wb(2, half)
-        second_product(0)
-        for half in range(2):
-            transpose_and_regroup_wb(3, half)
-            quantise_wb(3, half)
-            second_product(1 + half)
-        second_product(3)
+        second_product((0, 1))
+        copy_kv(on_scalar, (0, 1))
+        store_quarter(0, (nc.sync, nc.sync))
+        transpose_wb(6)
+        regroup_wb(on_vector, 5)
+        transpose_wb(7)
+        regroup_wb(on_scalar, 6)
+        quantise_wb(5)
+        second_product((2, 3))
+        regroup_wb(on_vector, 7)
+        copy_kv(on_scalar, (2, 3))
+        store_quarter(1, (nc.sync, nc.sync))
+        second_product((4, 5))
+        quantise_wb(6)
+        quantise_wb(7)
+        copy_kv(on_scalar, (4, 5))
+        store_quarter(2, (nc.sync, nc.sync))
+        second_product((6,))
+        second_product((7,))
+        copy_kv(on_vector, (6,))
+        copy_kv(on_scalar, (7,))
+        store_quarter(3, (nc.sync, nc.scalar))

@@ -127,6 +127,8 @@ def tile_modelnew_pb_s_kernel(
         table_warm = keep.tile([P, 1], F32)
         nc.scalar.activation(out=table_warm[:], in_=sin_cos[:, 1, 0:1], func=ACT.Abs_reciprocal_sqrt)
 
+        gain = keep.tile([P, CHUNKS], F32)
+        nc.gpsimd.tensor_copy(out=gain[:], in_=gain_bf[:])
         prod = keep.tile([P, 2, 2, ROPE_HALF], F32)
         nc.gpsimd.tensor_tensor(
             out=prod[:],
@@ -142,12 +144,10 @@ def tile_modelnew_pb_s_kernel(
             out=rope[:, ROPE_HALF:ROPE], in0=prod[:, 1, 1, :], in1=prod[:, 0, 0, :], op=ALU.add
         )
         for b in range(BATCH):
-            nc.sync.dma_start(
+            nc.gpsimd.dma_start(
                 out=key_s[b].rearrange("h s d -> s h d")[:, :, HALF_HEAD:HEAD_COLS],
                 in_=rope[b:P:BATCH, :].unsqueeze(1).to_broadcast([SEQ, HEADS, ROPE]),
             )
-        gain = keep.tile([P, CHUNKS], F32)
-        nc.gpsimd.tensor_copy(out=gain[:], in_=gain_bf[:])
 
         x_grouped = keep.tile([P, PASSES_1, TOK, PACK], BF16, align_bytes=64)
         x_codes = keep.tile([P, PASSES_1, TOK], U32, align_bytes=64)
@@ -160,20 +160,23 @@ def tile_modelnew_pb_s_kernel(
         wb_scales = keep.tile([P, PARTS * PART_ROWS], U8, align_bytes=64)
         squares = keep.tile([P, CHUNKS, TOK], F32)
         gained = keep.tile([P, CHUNKS, TOK], F32)
-        kv_sb = [keep.tile([P, 2 * PART_ROWS], F32, name=f"kv_sb_{q}") for q in range(PARTS // 2)]
+        groups = ((0, 1), (2, 3), (4, 5), (6, 7))
+        kv_sb = {}
+        for parts in groups:
+            kv_sb[parts] = keep.tile([P, PART_ROWS * len(parts)], F32, name="kv_sb_%d" % parts[0])
         banks = {}
         sum_sq = norm_psum.tile([P, TOK], F32)
 
-        def transpose_wa(t):
-            bank = staging.tile([P, PASSES_1, 2, P], F32, tag="bank")
-            for g in range(PASSES_1):
-                transpose_words(nc, bank[:, g], wa_sb[:, t, KR * g : KR * (g + 1)], ident[:])
-            banks["a", t] = bank
+        def transpose_wa(t, passes=(0, 1)):
+            bank = staging.tile([P, len(passes), 2, P], F32, tag="bank")
+            for i, g in enumerate(passes):
+                transpose_words(nc, bank[:, i], wa_sb[:, t, KR * g : KR * (g + 1)], ident[:])
+            banks["a", t, passes] = bank
 
-        def regroup_wa(copy_out, t):
+        def regroup_wa(copy_out, t, passes=(0, 1)):
             copy_out(
-                out=wa_grouped[:, t].bitcast(F32),
-                in_=banks["a", t][:].rearrange("p g u m -> p g m u"),
+                out=wa_grouped[:, t, passes[0] : passes[-1] + 1].bitcast(F32),
+                in_=banks["a", t, passes][:].rearrange("p g u m -> p g m u"),
             )
 
         def quantise_wa(t):
@@ -219,13 +222,9 @@ def tile_modelnew_pb_s_kernel(
                     stop=(g == PASSES_1 - 1),
                 )
 
-        def multiply_by_gain(pair):
-            chunks = slice(2 * pair, 2 * pair + 2)
-            nc.vector.tensor_tensor(
-                out=gained[:, chunks, :],
-                in0=ckv[pair][:],
-                in1=gain[:, chunks].unsqueeze(2).to_broadcast([P, 2, TOK]),
-                op=ALU.mult,
+        def multiply_by_gain(t):
+            nc.scalar.activation(
+                out=gained[:, t, :], in_=ckv[t // 2][:, t % 2, :], func=ACT.Copy, scale=gain[:, t : t + 1]
             )
 
         def add_over_partitions(values, start=False, stop=False):
@@ -246,24 +245,26 @@ def tile_modelnew_pb_s_kernel(
             banks["kv", parts] = kv_ps
 
         def copy_kv(copy_out, parts):
-            q, lo = parts[0] // 2, PART_ROWS * (parts[0] % 2)
+            group = [g for g in groups if parts[0] in g][0]
+            lo = PART_ROWS * (parts[0] - group[0])
             copy_out(
-                out=kv_sb[q][:, lo : lo + PART_ROWS * len(parts)].rearrange(
+                out=kv_sb[group][:, lo : lo + PART_ROWS * len(parts)].rearrange(
                     "p (h n i) -> p h n i", n=P, i=2
                 ),
                 in_=banks["kv", parts][:].rearrange("p (h i n) -> p h n i", n=P, i=2),
             )
 
-        def store_kv(q, b, queue):
-            heads = slice(HEADS_PER_QUARTER * q, HEADS_PER_QUARTER * (q + 1))
-            by_head = kv_sb[q][b:P:BATCH, :].rearrange("s (h c) -> s h c", c=HEAD_COLS)
-            queue.dma_start(
-                out=key_s[b, heads, :, 0:HALF_HEAD].rearrange("h s d -> s h d"),
-                in_=by_head[:, :, 0:HALF_HEAD],
-            )
-            queue.dma_start(
-                out=v[b, heads].rearrange("h s d -> s h d"), in_=by_head[:, :, HALF_HEAD:HEAD_COLS]
-            )
+        def store_kv(group, queues):
+            heads = slice(2 * group[0], 2 * group[-1] + 2)
+            for b in range(BATCH):
+                by_head = kv_sb[group][b:P:BATCH, :].rearrange("s (h c) -> s h c", c=HEAD_COLS)
+                queues[b].dma_start(
+                    out=key_s[b, heads, :, 0:HALF_HEAD].rearrange("h s d -> s h d"),
+                    in_=by_head[:, :, 0:HALF_HEAD],
+                )
+                queues[b].dma_start(
+                    out=v[b, heads].rearrange("h s d -> s h d"), in_=by_head[:, :, HALF_HEAD:HEAD_COLS]
+                )
 
         on_vector, on_scalar = nc.vector.tensor_copy, nc.scalar.copy
 
@@ -283,13 +284,15 @@ def tile_modelnew_pb_s_kernel(
         transpose_wa(0)
         regroup_wa(on_scalar, 0)
         transpose_wa(1)
-        regroup_wa(on_vector, 1)
+        regroup_wa(on_scalar, 1)
+        quantise_wa(0)
         transpose_wa(2)
         regroup_wa(on_scalar, 2)
-        transpose_wa(3)
-        quantise_wa(0)
         quantise_wa(1)
-        regroup_wa(on_vector, 3)
+        transpose_wa(3, (0,))
+        transpose_wa(3, (1,))
+        regroup_wa(on_vector, 3, (0,))
+        regroup_wa(on_scalar, 3, (1,))
         quantise_wa(2)
         quantise_wa(3)
 
@@ -302,27 +305,28 @@ def tile_modelnew_pb_s_kernel(
             out=squares_01[:], in0=squares[:, 0, :], in1=squares[:, 1, :], op=ALU.add
         )
         multiply_by_gain(0)
-        regroup_wb(on_scalar, 0)
-        transpose_wb(1)
+        multiply_by_gain(1)
+        regroup_wb(on_vector, 0)
+        transpose_wb(1, (0,))
         first_product(2)
         first_product(3)
         nc.scalar.activation(out=squares[:, 2, :], in_=ckv[1][:, 0, :], func=ACT.Square)
         nc.scalar.activation(out=squares[:, 3, :], in_=ckv[1][:, 1, :], func=ACT.Square)
-        quantise_wb(0)
-        multiply_by_gain(1)
-        regroup_wb(on_scalar, 1)
+        multiply_by_gain(2)
+        multiply_by_gain(3)
 
         add_over_partitions(squares_01[:], start=True)
-        transpose_wb(2, (0,))
+        transpose_wb(1, (1,))
+        regroup_wb(on_vector, 1)
         add_over_partitions(squares[:, 2, :])
         add_over_partitions(squares[:, 3, :], stop=True)
+        quantise_wb(0)
         rstd = keep.tile([P, TOK], F32)
         nc.scalar.activation(
             out=rstd[:], in_=sum_sq[:], func=ACT.Abs_reciprocal_sqrt, bias=eps[:, 0:1], scale=1.0 / KR
         )
-        transpose_wb(2, (1,))
+        transpose_wb(2)
         regroup_wb(on_scalar, 2)
-        quantise_wb(1)
         cn_grouped = keep.tile([P, TOK, PACK], BF16, align_bytes=64)
         nc.vector.tensor_tensor(
             out=cn_grouped[:],
@@ -330,7 +334,7 @@ def tile_modelnew_pb_s_kernel(
             in1=rstd[:].unsqueeze(2).to_broadcast([P, TOK, PACK]),
             op=ALU.mult,
         )
-        quantise_wb(2)
+        quantise_wb(1)
         cn_codes = keep.tile([P, TOK], U32, align_bytes=64)
         cn_scales = keep.tile([P, TOK], U8, align_bytes=64)
         nc.vector.quantize_mx(
@@ -340,35 +344,31 @@ def tile_modelnew_pb_s_kernel(
         )
         transpose_wb(3)
         regroup_wb(on_scalar, 3)
+        quantise_wb(2)
         transpose_wb(4)
         regroup_wb(on_vector, 4)
         quantise_wb(3)
-        transpose_wb(5)
-        quantise_wb(4)
-
-        def store_quarter(q, queues):
-            for b in range(BATCH):
-                store_kv(q, b, queues[b])
-
         second_product((0, 1))
         copy_kv(on_scalar, (0, 1))
-        store_quarter(0, (nc.sync, nc.sync))
-        transpose_wb(6)
-        regroup_wb(on_vector, 5)
-        transpose_wb(7)
-        regroup_wb(on_scalar, 6)
-        quantise_wb(5)
+        store_kv(groups[0], (nc.sync, nc.sync))
+        transpose_wb(5)
+        regroup_wb(on_scalar, 5)
+        quantise_wb(4)
         second_product((2, 3))
-        regroup_wb(on_vector, 7)
         copy_kv(on_scalar, (2, 3))
-        store_quarter(1, (nc.sync, nc.sync))
-        second_product((4, 5))
+        store_kv(groups[1], (nc.sync, nc.sync))
+        transpose_wb(6)
+        quantise_wb(5)
+        regroup_wb(on_vector, 6)
+        transpose_wb(7)
+        regroup_wb(on_scalar, 7)
         quantise_wb(6)
-        quantise_wb(7)
+        second_product((4, 5))
         copy_kv(on_scalar, (4, 5))
-        store_quarter(2, (nc.sync, nc.sync))
+        store_kv(groups[2], (nc.sync, nc.sync))
+        quantise_wb(7)
         second_product((6,))
         second_product((7,))
         copy_kv(on_vector, (6,))
         copy_kv(on_scalar, (7,))
-        store_quarter(3, (nc.sync, nc.scalar))
+        store_kv(groups[3], (nc.sync, nc.sync))

@@ -144,7 +144,7 @@ def tile_modelnew_pb_s_kernel(
             out=rope[:, ROPE_HALF:ROPE], in0=prod[:, 1, 1, :], in1=prod[:, 0, 0, :], op=ALU.add
         )
         for b in range(BATCH):
-            nc.gpsimd.dma_start(
+            nc.sync.dma_start(
                 out=key_s[b].rearrange("h s d -> s h d")[:, :, HALF_HEAD:HEAD_COLS],
                 in_=rope[b:P:BATCH, :].unsqueeze(1).to_broadcast([SEQ, HEADS, ROPE]),
             )

@@ -58,7 +58,7 @@ def tile_modelnew_pb_s_kernel(
             nc.sync.dma_start(out=wa_sb[:, t, :], in_=wa_rows[t])
         pe_sb = keep.tile([P, ROPE], BF16)
         for b in range(BATCH):
-            nc.sync.dma_start(out=pe_sb[b:P:BATCH, :], in_=k_pe_raw[b])
+            nc.scalar.dma_start(out=pe_sb[b:P:BATCH, :], in_=k_pe_raw[b])
         gain_bf = keep.tile([P, CHUNKS], BF16)
         nc.sync.dma_start(out=gain_bf[:], in_=kv_a_ln_w.rearrange("(p t) -> p t", t=CHUNKS))
         wb_sb = keep.tile([P, PARTS, 2, KR], BF16)
@@ -75,42 +75,45 @@ def tile_modelnew_pb_s_kernel(
         ones = keep.tile([P, P], F32)
         nc.vector.memset(ones[:], 1.0)
 
-        turn_rate = keep.tile([P, ROPE_HALF], F32)
-        for j in range(PACK):
-            nc.vector.tensor_scalar(
-                out=turn_rate[:, j : j + 1],
-                in0=ones[:, 0:1],
-                scalar1=THETA ** (-j / ROPE_HALF) / (2.0 * math.pi),
-                scalar2=None,
-                op0=ALU.mult,
-            )
+        phase = keep.tile([P, 2, ROPE_HALF], F32)
+        nc.vector.memset(phase[:, 0, :], 0.0)
+        ratio = keep.tile([P, ROPE_HALF], F32)
+        nc.vector.tensor_scalar(
+            out=ratio[:],
+            in0=ones[:, 0:ROPE_HALF],
+            scalar1=THETA ** (-1.0 / ROPE_HALF),
+            scalar2=None,
+            op0=ALU.mult,
+        )
+        nc.vector.memset(phase[:, 1, :], 0.25)
         pos_int = keep.tile([P, 1], I32)
         nc.vector.tensor_single_scalar(
             out=pos_int[:], in_=partition_no[:], scalar=1, op=ALU.arith_shift_right
         )
+        freq = keep.tile([P, ROPE_HALF], F32)
+        nc.vector.tensor_tensor_scan(
+            out=freq[:],
+            data0=ratio[:],
+            data1=phase[:, 0, :],
+            initial=THETA ** (1.0 / ROPE_HALF),
+            op0=ALU.mult,
+            op1=ALU.add,
+        )
+        pos_turns = keep.tile([P, 1], F32)
+        nc.vector.tensor_scalar(
+            out=pos_turns[:], in0=pos_int[:], scalar1=1.0 / (2.0 * math.pi), scalar2=None, op0=ALU.mult
+        )
         eps = keep.tile([P, 1], F32)
         nc.vector.tensor_scalar(out=eps[:], in0=ones[:, 0:1], scalar1=EPS, scalar2=None, op0=ALU.mult)
-        for j in range(PACK, ROPE_HALF, PACK):
-            nc.vector.tensor_scalar(
-                out=turn_rate[:, j : j + PACK],
-                in0=turn_rate[:, 0:PACK],
-                scalar1=THETA ** (-j / ROPE_HALF),
-                scalar2=None,
-                op0=ALU.mult,
-            )
-            if j == PACK:
-                pos = keep.tile([P, 1], F32)
-                nc.vector.tensor_copy(out=pos[:], in_=pos_int[:])
         turns = keep.tile([P, 2, ROPE_HALF], F32)
-        for i, quarter in enumerate((0.0, 0.25)):
-            nc.vector.tensor_scalar(
-                out=turns[:, i, :],
-                in0=turn_rate[:],
-                scalar1=pos[:, 0:1],
-                scalar2=quarter,
-                op0=ALU.mult,
-                op1=ALU.add,
-            )
+        nc.vector.scalar_tensor_tensor(
+            out=turns[:],
+            in0=freq[:].unsqueeze(1).to_broadcast([P, 2, ROPE_HALF]),
+            scalar=pos_turns[:, 0:1],
+            in1=phase[:],
+            op0=ALU.mult,
+            op1=ALU.add,
+        )
         whole = keep.tile([P, 2, ROPE_HALF], F32)
         nc.vector.tensor_scalar(
             out=whole[:],
@@ -125,7 +128,7 @@ def tile_modelnew_pb_s_kernel(
         sin_cos = keep.tile([P, 2, ROPE_HALF], F32)
         nc.scalar.activation(out=sin_cos[:], in_=frac[:], func=ACT.Sin, scale=2.0 * math.pi)
         table_warm = keep.tile([P, 1], F32)
-        nc.scalar.activation(out=table_warm[:], in_=sin_cos[:, 1, 0:1], func=ACT.Abs_reciprocal_sqrt)
+        nc.scalar.activation(out=table_warm[:], in_=ones[:, 0:1], func=ACT.Abs_reciprocal_sqrt)
 
         gain = keep.tile([P, CHUNKS], F32)
         nc.gpsimd.tensor_copy(out=gain[:], in_=gain_bf[:])
@@ -222,9 +225,18 @@ def tile_modelnew_pb_s_kernel(
                     stop=(g == PASSES_1 - 1),
                 )
 
-        def multiply_by_gain(t):
+        def multiply_by_gain(pair):
+            chunks = slice(2 * pair, 2 * pair + 2)
+            nc.vector.tensor_tensor(
+                out=gained[:, chunks, :],
+                in0=ckv[pair][:],
+                in1=gain[:, chunks].unsqueeze(2).to_broadcast([P, 2, TOK]),
+                op=ALU.mult,
+            )
+
+        def square(pair):
             nc.scalar.activation(
-                out=gained[:, t, :], in_=ckv[t // 2][:, t % 2, :], func=ACT.Copy, scale=gain[:, t : t + 1]
+                out=squares[:, 2 * pair : 2 * pair + 2, :], in_=ckv[pair][:], func=ACT.Square
             )
 
         def add_over_partitions(values, start=False, stop=False):
@@ -276,51 +288,43 @@ def tile_modelnew_pb_s_kernel(
                 out=x_grouped[:, g].bitcast(F32).rearrange("p (s b) u -> p s b u", b=BATCH),
                 in_=x_bank[:, g].rearrange("p u (b s) -> p s b u", b=BATCH),
             )
+        transpose_wa(0)
+        regroup_wa(on_vector, 0)
         nc.vector.quantize_mx(
             out=x_codes[:].rearrange("p g r -> p (g r)").bitcast(FP8X4),
             scales=x_scales[:].rearrange("p g r -> p (g r)"),
             in_=x_grouped[:].rearrange("p g r k -> p (g r k)"),
         )
-        transpose_wa(0)
-        regroup_wa(on_scalar, 0)
         transpose_wa(1)
         regroup_wa(on_scalar, 1)
         quantise_wa(0)
         transpose_wa(2)
         regroup_wa(on_scalar, 2)
-        quantise_wa(1)
         transpose_wa(3, (0,))
         transpose_wa(3, (1,))
+        quantise_wa(1)
         regroup_wa(on_vector, 3, (0,))
         regroup_wa(on_scalar, 3, (1,))
         quantise_wa(2)
-        quantise_wa(3)
-
         first_product(0)
         first_product(1)
-        nc.scalar.activation(out=squares[:, 0:2], in_=ckv[0][:], func=ACT.Square)
         transpose_wb(0)
-        squares_01 = keep.tile([P, TOK], F32)
-        nc.vector.tensor_tensor(
-            out=squares_01[:], in0=squares[:, 0, :], in1=squares[:, 1, :], op=ALU.add
-        )
-        multiply_by_gain(0)
-        multiply_by_gain(1)
-        regroup_wb(on_vector, 0)
-        transpose_wb(1, (0,))
+        quantise_wa(3)
         first_product(2)
         first_product(3)
-        nc.scalar.activation(out=squares[:, 2, :], in_=ckv[1][:, 0, :], func=ACT.Square)
-        nc.scalar.activation(out=squares[:, 3, :], in_=ckv[1][:, 1, :], func=ACT.Square)
-        multiply_by_gain(2)
-        multiply_by_gain(3)
-
+        square(0)
+        regroup_wb(on_vector, 0)
+        square(1)
+        transpose_wb(1)
+        squares_01 = keep.tile([P, TOK], F32)
+        nc.vector.tensor_tensor(out=squares_01[:], in0=squares[:, 0, :], in1=squares[:, 1, :], op=ALU.add)
+        multiply_by_gain(0)
         add_over_partitions(squares_01[:], start=True)
-        transpose_wb(1, (1,))
-        regroup_wb(on_vector, 1)
         add_over_partitions(squares[:, 2, :])
         add_over_partitions(squares[:, 3, :], stop=True)
+        multiply_by_gain(1)
         quantise_wb(0)
+        regroup_wb(on_scalar, 1)
         rstd = keep.tile([P, TOK], F32)
         nc.scalar.activation(
             out=rstd[:], in_=sum_sq[:], func=ACT.Abs_reciprocal_sqrt, bias=eps[:, 0:1], scale=1.0 / KR

@@ -75,6 +75,14 @@ def tile_modelnew_pb_s_kernel(
         ones = keep.tile([P, P], F32)
         nc.vector.memset(ones[:], 1.0)
 
+        sum_sq = norm_psum.tile([P, TOK], F32)
+
+        def keep_tensor_busy(times):
+            for n in range(times):
+                nc.tensor.matmul(out=sum_sq[:], lhsT=ones[:], rhs=ones[:], start=True, stop=True)
+
+        keep_tensor_busy(3)
+
         phase = keep.tile([P, 2, ROPE_HALF], F32)
         nc.vector.memset(phase[:, 0, :], 0.0)
         ratio = keep.tile([P, ROPE_HALF], F32)
@@ -168,7 +176,6 @@ def tile_modelnew_pb_s_kernel(
         for parts in groups:
             kv_sb[parts] = keep.tile([P, PART_ROWS * len(parts)], F32, name="kv_sb_%d" % parts[0])
         banks = {}
-        sum_sq = norm_psum.tile([P, TOK], F32)
 
         def transpose_wa(t, passes=(0, 1)):
             bank = staging.tile([P, len(passes), 2, P], F32, tag="bank")
@@ -302,6 +309,7 @@ def tile_modelnew_pb_s_kernel(
         regroup_wa(on_scalar, 2)
         transpose_wa(3, (0,))
         transpose_wa(3, (1,))
+        keep_tensor_busy(2)
         quantise_wa(1)
         regroup_wa(on_vector, 3, (0,))
         regroup_wa(on_scalar, 3, (1,))
@@ -331,6 +339,7 @@ def tile_modelnew_pb_s_kernel(
         )
         transpose_wb(2)
         regroup_wb(on_scalar, 2)
+        quantise_wb(1)
         cn_grouped = keep.tile([P, TOK, PACK], BF16, align_bytes=64)
         nc.vector.tensor_tensor(
             out=cn_grouped[:],
@@ -338,7 +347,6 @@ def tile_modelnew_pb_s_kernel(
             in1=rstd[:].unsqueeze(2).to_broadcast([P, TOK, PACK]),
             op=ALU.mult,
         )
-        quantise_wb(1)
         cn_codes = keep.tile([P, TOK], U32, align_bytes=64)
         cn_scales = keep.tile([P, TOK], U8, align_bytes=64)
         nc.vector.quantize_mx(

@@ -81,7 +81,7 @@ def tile_modelnew_pb_s_kernel(
             for n in range(times):
                 nc.tensor.matmul(out=sum_sq[:], lhsT=ones[:], rhs=ones[:], start=True, stop=True)
 
-        keep_tensor_busy(3)
+        keep_tensor_busy(4)
 
         phase = keep.tile([P, 2, ROPE_HALF], F32)
         nc.vector.memset(phase[:, 0, :], 0.0)
@@ -249,9 +249,28 @@ def tile_modelnew_pb_s_kernel(
         def add_over_partitions(values, start=False, stop=False):
             nc.tensor.matmul(out=sum_sq[:], lhsT=ones[:], rhs=values, start=start, stop=stop)
 
+        def keep_tensor_busy_mx(out, times):
+            n = out.shape[1]
+            rhs, rhs_scale = (wb_codes, wb_scales) if n > 2 * TOK else (x_codes, x_scales)
+            if n <= 2 * TOK:
+                rhs = rhs[:].rearrange("p g r -> p (g r)")
+                rhs_scale = rhs_scale[:].rearrange("p g r -> p (g r)")
+            for i in range(times):
+                nc.tensor.matmul_mx(
+                    out=out,
+                    lhsT=x_codes[:, 0, :].bitcast(FP8X4),
+                    lhsT_scale=x_scales[:, 0, :],
+                    rhs=rhs[:, 0:n].bitcast(FP8X4),
+                    rhs_scale=rhs_scale[:, 0:n],
+                    start=True,
+                    stop=True,
+                )
+
         def second_product(parts):
             cols = slice(PART_ROWS * parts[0], PART_ROWS * (parts[-1] + 1))
             kv_ps = products.tile([P, PART_ROWS * len(parts)], F32, tag="product")
+            if parts[0] < 4:
+                keep_tensor_busy_mx(kv_ps[:], 1)
             nc.tensor.matmul_mx(
                 out=kv_ps[:],
                 lhsT=cn_codes[:].bitcast(FP8X4),
@@ -296,6 +315,7 @@ def tile_modelnew_pb_s_kernel(
                 in_=x_bank[:, g].rearrange("p u (b s) -> p s b u", b=BATCH),
             )
         transpose_wa(0)
+        keep_tensor_busy(2)
         regroup_wa(on_vector, 0)
         nc.vector.quantize_mx(
             out=x_codes[:].rearrange("p g r -> p (g r)").bitcast(FP8X4),
@@ -309,7 +329,7 @@ def tile_modelnew_pb_s_kernel(
         regroup_wa(on_scalar, 2)
         transpose_wa(3, (0,))
         transpose_wa(3, (1,))
-        keep_tensor_busy(2)
+        keep_tensor_busy_mx(ckv_01[:].rearrange("p c r -> p (c r)"), 2)
         quantise_wa(1)
         regroup_wa(on_vector, 3, (0,))
         regroup_wa(on_scalar, 3, (1,))

@@ -25,7 +25,7 @@ PASSES_1 = D // (P * PACK)
 CHUNKS = KR // P
 PARTS = 8
 PART_ROWS = HEADS * HEAD_COLS // PARTS
-HEADS_PER_QUARTER = 4
+WB_LOADS = ((0,), (1,), (2, 3), (4, 5), (6, 7))
 EPS = 1e-6
 THETA = 10000.0
 ROUND_MAGIC = 12582912.0
@@ -51,7 +51,10 @@ def tile_modelnew_pb_s_kernel(
         ctx.enter_context(tc.manual_schedule())
 
         x_sb = keep.tile([P, D], BF16)
-        nc.sync.dma_start(out=x_sb[:], in_=hidden_states.flatten_outer_dims())
+        x_rows = hidden_states.flatten_outer_dims()
+        for g in range(PASSES_1):
+            pass_cols = slice(KR * g, KR * (g + 1))
+            nc.sync.dma_start(out=x_sb[:, pass_cols], in_=x_rows[:, pass_cols])
         wa_sb = keep.tile([P, CHUNKS, D], BF16)
         wa_rows = kv_a_w_ckv.rearrange("(p t) k -> t p k", t=CHUNKS)
         for t in range(CHUNKS):
@@ -63,10 +66,9 @@ def tile_modelnew_pb_s_kernel(
         nc.sync.dma_start(out=gain_bf[:], in_=kv_a_ln_w.rearrange("(p t) -> p t", t=CHUNKS))
         wb_sb = keep.tile([P, PARTS, 2, KR], BF16)
         wb_rows = kv_b_w.rearrange("(m p i) k -> p m (i k)", m=PARTS, i=2)
-        for m in range(0, PARTS, 2):
-            nc.sync.dma_start(
-                out=wb_sb[:, m : m + 2].rearrange("p m i k -> p m (i k)"), in_=wb_rows[:, m : m + 2]
-            )
+        for parts in WB_LOADS:
+            ms = slice(parts[0], parts[-1] + 1)
+            nc.sync.dma_start(out=wb_sb[:, ms].rearrange("p m i k -> p m (i k)"), in_=wb_rows[:, ms])
 
         partition_no = keep.tile([P, 1], I32)
         nc.gpsimd.iota(partition_no[:], pattern=[[0, 1]], base=0, channel_multiplier=1)
@@ -82,6 +84,9 @@ def tile_modelnew_pb_s_kernel(
                 nc.tensor.matmul(out=sum_sq[:], lhsT=ones[:], rhs=ones[:], start=True, stop=True)
 
         keep_tensor_busy(4)
+
+        table_warm = keep.tile([P, 2], F32)
+        nc.scalar.activation(out=table_warm[:, 0:1], in_=ones[:, 0:1], func=ACT.Sin)
 
         phase = keep.tile([P, 2, ROPE_HALF], F32)
         nc.vector.memset(phase[:, 0, :], 0.0)
@@ -135,8 +140,7 @@ def tile_modelnew_pb_s_kernel(
         nc.vector.tensor_tensor(out=frac[:], in0=turns[:], in1=whole[:], op=ALU.subtract)
         sin_cos = keep.tile([P, 2, ROPE_HALF], F32)
         nc.scalar.activation(out=sin_cos[:], in_=frac[:], func=ACT.Sin, scale=2.0 * math.pi)
-        table_warm = keep.tile([P, 1], F32)
-        nc.scalar.activation(out=table_warm[:], in_=ones[:, 0:1], func=ACT.Abs_reciprocal_sqrt)
+        nc.scalar.activation(out=table_warm[:, 1:2], in_=ones[:, 0:1], func=ACT.Abs_reciprocal_sqrt)
 
         gain = keep.tile([P, CHUNKS], F32)
         nc.gpsimd.tensor_copy(out=gain[:], in_=gain_bf[:])
@@ -217,13 +221,15 @@ def tile_modelnew_pb_s_kernel(
             )
 
         ckv_01 = products.tile([P, 2, TOK], F32, tag="product")
-        ckv_23 = products.tile([P, 2, TOK], F32, tag="product")
-        ckv = [ckv_01, ckv_23]
+        ckv_2 = products.tile([P, 1, TOK], F32, tag="product")
+        ckv_3 = products.tile([P, 1, TOK], F32, tag="product")
+        ckv = {(0, 1): ckv_01, (2,): ckv_2, (3,): ckv_3}
+        ckv_of_chunk = [ckv_01[:, 0, :], ckv_01[:, 1, :], ckv_2[:, 0, :], ckv_3[:, 0, :]]
 
         def first_product(t):
             for g in range(PASSES_1):
                 nc.tensor.matmul_mx(
-                    out=ckv[t // 2][:, t % 2, :],
+                    out=ckv_of_chunk[t],
                     lhsT=wa_codes[:, t, g, :].bitcast(FP8X4),
                     lhsT_scale=wa_scales[:, t, g, :],
                     rhs=x_codes[:, g, :].bitcast(FP8X4),
@@ -232,19 +238,19 @@ def tile_modelnew_pb_s_kernel(
                     stop=(g == PASSES_1 - 1),
                 )
 
-        def multiply_by_gain(pair):
-            chunks = slice(2 * pair, 2 * pair + 2)
+        def multiply_by_gain(chunks):
+            n = len(chunks)
+            at = slice(chunks[0], chunks[0] + n)
             nc.vector.tensor_tensor(
-                out=gained[:, chunks, :],
-                in0=ckv[pair][:],
-                in1=gain[:, chunks].unsqueeze(2).to_broadcast([P, 2, TOK]),
+                out=gained[:, at, :],
+                in0=ckv[chunks][:],
+                in1=gain[:, at].unsqueeze(2).to_broadcast([P, n, TOK]),
                 op=ALU.mult,
             )
 
-        def square(pair):
-            nc.scalar.activation(
-                out=squares[:, 2 * pair : 2 * pair + 2, :], in_=ckv[pair][:], func=ACT.Square
-            )
+        def square(chunks):
+            at = slice(chunks[0], chunks[0] + len(chunks))
+            nc.scalar.activation(out=squares[:, at, :], in_=ckv[chunks][:], func=ACT.Square)
 
         def add_over_partitions(values, start=False, stop=False):
             nc.tensor.matmul(out=sum_sq[:], lhsT=ones[:], rhs=values, start=start, stop=stop)
@@ -306,51 +312,51 @@ def tile_modelnew_pb_s_kernel(
 
         on_vector, on_scalar = nc.vector.tensor_copy, nc.scalar.copy
 
-        x_bank = staging.tile([P, PASSES_1, 2, TOK], F32, tag="bank")
-        for g in range(PASSES_1):
-            transpose_words(nc, x_bank[:, g], x_sb[:, KR * g : KR * (g + 1)], ident[:])
-        for g in range(PASSES_1):
-            nc.vector.tensor_copy(
+        for g, copy_out in ((0, on_vector), (1, on_scalar)):
+            x_bank = staging.tile([P, 2, TOK], F32, tag="bank")
+            transpose_words(nc, x_bank[:], x_sb[:, KR * g : KR * (g + 1)], ident[:])
+            copy_out(
                 out=x_grouped[:, g].bitcast(F32).rearrange("p (s b) u -> p s b u", b=BATCH),
-                in_=x_bank[:, g].rearrange("p u (b s) -> p s b u", b=BATCH),
+                in_=x_bank[:].rearrange("p u (b s) -> p s b u", b=BATCH),
             )
         transpose_wa(0)
-        keep_tensor_busy(2)
         regroup_wa(on_vector, 0)
+        transpose_wa(1)
+        regroup_wa(on_scalar, 1)
         nc.vector.quantize_mx(
             out=x_codes[:].rearrange("p g r -> p (g r)").bitcast(FP8X4),
             scales=x_scales[:].rearrange("p g r -> p (g r)"),
             in_=x_grouped[:].rearrange("p g r k -> p (g r k)"),
         )
-        transpose_wa(1)
-        regroup_wa(on_scalar, 1)
         quantise_wa(0)
         transpose_wa(2)
         regroup_wa(on_scalar, 2)
-        transpose_wa(3, (0,))
-        transpose_wa(3, (1,))
-        keep_tensor_busy_mx(ckv_01[:].rearrange("p c r -> p (c r)"), 2)
         quantise_wa(1)
+        transpose_wa(3, (0,))
         regroup_wa(on_vector, 3, (0,))
+        transpose_wa(3, (1,))
         regroup_wa(on_scalar, 3, (1,))
+        keep_tensor_busy_mx(ckv_01[:].rearrange("p c r -> p (c r)"), 2)
         quantise_wa(2)
         first_product(0)
         first_product(1)
         transpose_wb(0)
         quantise_wa(3)
+        square((0, 1))
         first_product(2)
         first_product(3)
-        square(0)
         regroup_wb(on_vector, 0)
-        square(1)
-        transpose_wb(1)
+        square((2,))
+        square((3,))
         squares_01 = keep.tile([P, TOK], F32)
-        nc.vector.tensor_tensor(out=squares_01[:], in0=squares[:, 0, :], in1=squares[:, 1, :], op=ALU.add)
-        multiply_by_gain(0)
+        nc.gpsimd.tensor_tensor(out=squares_01[:], in0=squares[:, 0, :], in1=squares[:, 1, :], op=ALU.add)
+        transpose_wb(1)
         add_over_partitions(squares_01[:], start=True)
         add_over_partitions(squares[:, 2, :])
         add_over_partitions(squares[:, 3, :], stop=True)
-        multiply_by_gain(1)
+        multiply_by_gain((0, 1))
+        multiply_by_gain((2,))
+        multiply_by_gain((3,))
         quantise_wb(0)
         regroup_wb(on_scalar, 1)
         rstd = keep.tile([P, TOK], F32)

@@ -50,6 +50,11 @@ def tile_modelnew_pb_s_kernel(
         norm_psum = ctx.enter_context(tc.psum_pool(name="norm_psum", bufs=1))
         ctx.enter_context(tc.manual_schedule())
 
+        pe_sb = keep.tile([P, ROPE], BF16)
+        for b in range(BATCH):
+            nc.scalar.dma_start(out=pe_sb[b:P:BATCH, :], in_=k_pe_raw[b])
+        gain_bf = keep.tile([P, CHUNKS], BF16)
+        nc.scalar.dma_start(out=gain_bf[:], in_=kv_a_ln_w.rearrange("(p t) -> p t", t=CHUNKS))
         x_sb = keep.tile([P, D], BF16)
         x_rows = hidden_states.flatten_outer_dims()
         for g in range(PASSES_1):
@@ -59,11 +64,6 @@ def tile_modelnew_pb_s_kernel(
         wa_rows = kv_a_w_ckv.rearrange("(p t) k -> t p k", t=CHUNKS)
         for t in range(CHUNKS):
             nc.sync.dma_start(out=wa_sb[:, t, :], in_=wa_rows[t])
-        pe_sb = keep.tile([P, ROPE], BF16)
-        for b in range(BATCH):
-            nc.scalar.dma_start(out=pe_sb[b:P:BATCH, :], in_=k_pe_raw[b])
-        gain_bf = keep.tile([P, CHUNKS], BF16)
-        nc.sync.dma_start(out=gain_bf[:], in_=kv_a_ln_w.rearrange("(p t) -> p t", t=CHUNKS))
         wb_sb = keep.tile([P, PARTS, 2, KR], BF16)
         wb_rows = kv_b_w.rearrange("(m p i) k -> p m (i k)", m=PARTS, i=2)
         for parts in WB_LOADS:
@@ -345,16 +345,16 @@ def tile_modelnew_pb_s_kernel(
         square((0, 1))
         first_product(2)
         first_product(3)
+        multiply_by_gain((0, 1))
         regroup_wb(on_vector, 0)
+        squares_01 = keep.tile([P, TOK], F32)
+        nc.vector.tensor_tensor(out=squares_01[:], in0=squares[:, 0, :], in1=squares[:, 1, :], op=ALU.add)
         square((2,))
         square((3,))
-        squares_01 = keep.tile([P, TOK], F32)
-        nc.gpsimd.tensor_tensor(out=squares_01[:], in0=squares[:, 0, :], in1=squares[:, 1, :], op=ALU.add)
         transpose_wb(1)
-        add_over_partitions(squares_01[:], start=True)
-        add_over_partitions(squares[:, 2, :])
-        add_over_partitions(squares[:, 3, :], stop=True)
-        multiply_by_gain((0, 1))
+        add_over_partitions(squares[:, 2, :], start=True)
+        add_over_partitions(squares[:, 3, :])
+        add_over_partitions(squares_01[:], stop=True)
         multiply_by_gain((2,))
         multiply_by_gain((3,))
         quantise_wb(0)

@@ -319,8 +319,10 @@ def tile_modelnew_pb_s_kernel(
                 out=x_grouped[:, g].bitcast(F32).rearrange("p (s b) u -> p s b u", b=BATCH),
                 in_=x_bank[:].rearrange("p u (b s) -> p s b u", b=BATCH),
             )
+        keep_tensor_busy(1)
         transpose_wa(0)
         regroup_wa(on_vector, 0)
+        keep_tensor_busy(1)
         transpose_wa(1)
         regroup_wa(on_scalar, 1)
         nc.vector.quantize_mx(

import math
from contextlib import ExitStack

import concourse.mybir as mybir
from concourse.masks import make_identity

F32 = mybir.dt.float32
BF16 = mybir.dt.bfloat16
U32 = mybir.dt.uint32
U8 = mybir.dt.uint8
I32 = mybir.dt.int32
FP8X4 = mybir.dt.float8_e4m3fn_x4
ACT = mybir.ActivationFunctionType
ALU = mybir.AluOpType

P = 128
PACK = 4
BATCH, SEQ = 2, 64
TOK = BATCH * SEQ
D = 1024
KR = 512
HEADS, HEAD_COLS, HALF_HEAD = 16, 128, 64
ROPE, ROPE_HALF = 64, 32
PASSES_1 = D // (P * PACK)
CHUNKS = KR // P
PARTS = 8
PART_ROWS = HEADS * HEAD_COLS // PARTS
WB_LOADS = ((0,), (1,), (2, 3), (4, 5), (6, 7))
EPS = 1e-6
THETA = 10000.0
ROUND_MAGIC = 12582912.0

FLOPS = 2 * TOK * D * KR + 2 * TOK * KR * HEADS * HEAD_COLS


def transpose_words(nc, bank, rows_bf16, ident):
    words = rows_bf16.bitcast(F32)
    for u in range(2):
        nc.tensor.transpose(bank[:, u, :], words[:, u::2], ident)


def tile_modelnew_pb_s_kernel(
    tc, hidden_states, kv_a_w_ckv, k_pe_raw, kv_a_ln_w, kv_b_w, key_s, v
):
    nc = tc.nc
    with ExitStack() as ctx:
        keep = ctx.enter_context(tc.tile_pool(name="keep", bufs=1))
        staging = ctx.enter_context(tc.psum_pool(name="staging", bufs=4))
        products = ctx.enter_context(tc.psum_pool(name="products", bufs=3))
        norm_psum = ctx.enter_context(tc.psum_pool(name="norm_psum", bufs=1))
        ctx.enter_context(tc.manual_schedule())

        pe_sb = keep.tile([P, ROPE], BF16)
        for b in range(BATCH):
            nc.scalar.dma_start(out=pe_sb[b:P:BATCH, :], in_=k_pe_raw[b])
        gain_bf = keep.tile([P, CHUNKS], BF16)
        nc.scalar.dma_start(out=gain_bf[:], in_=kv_a_ln_w.rearrange("(p t) -> p t", t=CHUNKS))
        x_sb = keep.tile([P, D], BF16)
        x_rows = hidden_states.flatten_outer_dims()
        for g in range(PASSES_1):
            pass_cols = slice(KR * g, KR * (g + 1))
            nc.sync.dma_start(out=x_sb[:, pass_cols], in_=x_rows[:, pass_cols])
        wa_sb = keep.tile([P, CHUNKS, D], BF16)
        wa_rows = kv_a_w_ckv.rearrange("(p t) k -> t p k", t=CHUNKS)
        for t in range(CHUNKS):
            nc.sync.dma_start(out=wa_sb[:, t, :], in_=wa_rows[t])
        wb_sb = keep.tile([P, PARTS, 2, KR], BF16)
        wb_rows = kv_b_w.rearrange("(m p i) k -> p m (i k)", m=PARTS, i=2)
        for parts in WB_LOADS:
            ms = slice(parts[0], parts[-1] + 1)
            nc.sync.dma_start(out=wb_sb[:, ms].rearrange("p m i k -> p m (i k)"), in_=wb_rows[:, ms])

        partition_no = keep.tile([P, 1], I32)
        nc.gpsimd.iota(partition_no[:], pattern=[[0, 1]], base=0, channel_multiplier=1)
        ident = keep.tile([P, P], F32)
        make_identity(nc, ident[:])
        ones = keep.tile([P, P], F32)
        nc.vector.memset(ones[:], 1.0)

        sum_sq = norm_psum.tile([P, TOK], F32)

        def keep_tensor_busy(times):
            for n in range(times):
                nc.tensor.matmul(out=sum_sq[:], lhsT=ones[:], rhs=ones[:], start=True, stop=True)

        keep_tensor_busy(4)

        table_warm = keep.tile([P, 2], F32)
        nc.scalar.activation(out=table_warm[:, 0:1], in_=ones[:, 0:1], func=ACT.Sin)

        phase = keep.tile([P, 2, ROPE_HALF], F32)
        nc.vector.memset(phase[:, 0, :], 0.0)
        ratio = keep.tile([P, ROPE_HALF], F32)
        nc.vector.tensor_scalar(
            out=ratio[:],
            in0=ones[:, 0:ROPE_HALF],
            scalar1=THETA ** (-1.0 / ROPE_HALF),
            scalar2=None,
            op0=ALU.mult,
        )
        nc.vector.memset(phase[:, 1, :], 0.25)
        pos_int = keep.tile([P, 1], I32)
        nc.vector.tensor_single_scalar(
            out=pos_int[:], in_=partition_no[:], scalar=1, op=ALU.arith_shift_right
        )
        freq = keep.tile([P, ROPE_HALF], F32)
        nc.vector.tensor_tensor_scan(
            out=freq[:],
            data0=ratio[:],
            data1=phase[:, 0, :],
            initial=THETA ** (1.0 / ROPE_HALF),
            op0=ALU.mult,
            op1=ALU.add,
        )
        pos_turns = keep.tile([P, 1], F32)
        nc.vector.tensor_scalar(
            out=pos_turns[:], in0=pos_int[:], scalar1=1.0 / (2.0 * math.pi), scalar2=None, op0=ALU.mult
        )
        eps = keep.tile([P, 1], F32)
        nc.vector.tensor_scalar(out=eps[:], in0=ones[:, 0:1], scalar1=EPS, scalar2=None, op0=ALU.mult)
        turns = keep.tile([P, 2, ROPE_HALF], F32)
        nc.vector.scalar_tensor_tensor(
            out=turns[:],
            in0=freq[:].unsqueeze(1).to_broadcast([P, 2, ROPE_HALF]),
            scalar=pos_turns[:, 0:1],
            in1=phase[:],
            op0=ALU.mult,
            op1=ALU.add,
        )
        whole = keep.tile([P, 2, ROPE_HALF], F32)
        nc.vector.tensor_scalar(
            out=whole[:],
            in0=turns[:],
            scalar1=ROUND_MAGIC,
            scalar2=ROUND_MAGIC,
            op0=ALU.add,
            op1=ALU.subtract,
        )
        frac = keep.tile([P, 2, ROPE_HALF], F32)
        nc.vector.tensor_tensor(out=frac[:], in0=turns[:], in1=whole[:], op=ALU.subtract)
        sin_cos = keep.tile([P, 2, ROPE_HALF], F32)
        nc.scalar.activation(out=sin_cos[:], in_=frac[:], func=ACT.Sin, scale=2.0 * math.pi)
        nc.scalar.activation(out=table_warm[:, 1:2], in_=ones[:, 0:1], func=ACT.Abs_reciprocal_sqrt)

        gain = keep.tile([P, CHUNKS], F32)
        nc.gpsimd.tensor_copy(out=gain[:], in_=gain_bf[:])
        prod = keep.tile([P, 2, 2, ROPE_HALF], F32)
        nc.gpsimd.tensor_tensor(
            out=prod[:],
            in0=pe_sb[:].rearrange("p (h j) -> p h j", h=2).unsqueeze(1).to_broadcast([P, 2, 2, ROPE_HALF]),
            in1=sin_cos[:].unsqueeze(2).to_broadcast([P, 2, 2, ROPE_HALF]),
            op=ALU.mult,
        )
        rope = keep.tile([P, ROPE], F32)
        nc.gpsimd.tensor_tensor(
            out=rope[:, 0:ROPE_HALF], in0=prod[:, 1, 0, :], in1=prod[:, 0, 1, :], op=ALU.subtract
        )
        nc.gpsimd.tensor_tensor(
            out=rope[:, ROPE_HALF:ROPE], in0=prod[:, 1, 1, :], in1=prod[:, 0, 0, :], op=ALU.add
        )
        for b in range(BATCH):
            nc.sync.dma_start(
                out=key_s[b].rearrange("h s d -> s h d")[:, :, HALF_HEAD:HEAD_COLS],
                in_=rope[b:P:BATCH, :].unsqueeze(1).to_broadcast([SEQ, HEADS, ROPE]),
            )

        x_grouped = keep.tile([P, PASSES_1, TOK, PACK], BF16, align_bytes=64)
        x_codes = keep.tile([P, PASSES_1, TOK], U32, align_bytes=64)
        x_scales = keep.tile([P, PASSES_1, TOK], U8, align_bytes=64)
        wa_grouped = keep.tile([P, CHUNKS, PASSES_1, P, PACK], BF16, align_bytes=64)
        wa_codes = keep.tile([P, CHUNKS, PASSES_1, P], U32, align_bytes=64)
        wa_scales = keep.tile([P, CHUNKS, PASSES_1, P], U8, align_bytes=64)
        wb_grouped = keep.tile([P, PARTS, PART_ROWS, PACK], BF16, align_bytes=64)
        wb_codes = keep.tile([P, PARTS * PART_ROWS], U32, align_bytes=64)
        wb_scales = keep.tile([P, PARTS * PART_ROWS], U8, align_bytes=64)
        squares = keep.tile([P, CHUNKS, TOK], F32)
        gained = keep.tile([P, CHUNKS, TOK], F32)
        groups = ((0, 1), (2, 3), (4, 5), (6, 7))
        kv_sb = {}
        for parts in groups:
            kv_sb[parts] = keep.tile([P, PART_ROWS * len(parts)], F32, name="kv_sb_%d" % parts[0])
        banks = {}

        def transpose_wa(t, passes=(0, 1)):
            bank = staging.tile([P, len(passes), 2, P], F32, tag="bank")
            for i, g in enumerate(passes):
                transpose_words(nc, bank[:, i], wa_sb[:, t, KR * g : KR * (g + 1)], ident[:])
            banks["a", t, passes] = bank

        def regroup_wa(copy_out, t, passes=(0, 1)):
            copy_out(
                out=wa_grouped[:, t, passes[0] : passes[-1] + 1].bitcast(F32),
                in_=banks["a", t, passes][:].rearrange("p g u m -> p g m u"),
            )

        def quantise_wa(t):
            nc.vector.quantize_mx(
                out=wa_codes[:, t].rearrange("p g m -> p (g m)").bitcast(FP8X4),
                scales=wa_scales[:, t].rearrange("p g m -> p (g m)"),
                in_=wa_grouped[:, t].rearrange("p g m k -> p (g m k)"),
            )

        def transpose_wb(m, rows=(0, 1)):
            if 0 in rows:
                banks["b", m] = staging.tile([P, 2, 2, P], F32, tag="bank", name="wb_bank")
            for i in rows:
                transpose_words(nc, banks["b", m][:, i], wb_sb[:, m, i, :], ident[:])

        def regroup_wb(copy_out, m):
            copy_out(
                out=wb_grouped[:, m].bitcast(F32).rearrange("p (i n) u -> p i n u", i=2),
                in_=banks["b", m][:].rearrange("p i u n -> p i n u"),
            )

        def quantise_wb(m):
            cols = slice(PART_ROWS * m, PART_ROWS * (m + 1))
            nc.vector.quantize_mx(
                out=wb_codes[:, cols].bitcast(FP8X4),
                scales=wb_scales[:, cols],
                in_=wb_grouped[:, m].rearrange("p c k -> p (c k)"),
            )

        ckv_01 = products.tile([P, 2, TOK], F32, tag="product")
        ckv_2 = products.tile([P, 1, TOK], F32, tag="product")
        ckv_3 = products.tile([P, 1, TOK], F32, tag="product")
        ckv = {(0, 1): ckv_01, (2,): ckv_2, (3,): ckv_3}
        ckv_of_chunk = [ckv_01[:, 0, :], ckv_01[:, 1, :], ckv_2[:, 0, :], ckv_3[:, 0, :]]

        def first_product(t):
            for g in range(PASSES_1):
                nc.tensor.matmul_mx(
                    out=ckv_of_chunk[t],
                    lhsT=wa_codes[:, t, g, :].bitcast(FP8X4),
                    lhsT_scale=wa_scales[:, t, g, :],
                    rhs=x_codes[:, g, :].bitcast(FP8X4),
                    rhs_scale=x_scales[:, g, :],
                    start=(g == 0),
                    stop=(g == PASSES_1 - 1),
                )

        def multiply_by_gain(chunks):
            n = len(chunks)
            at = slice(chunks[0], chunks[0] + n)
            nc.vector.tensor_tensor(
                out=gained[:, at, :],
                in0=ckv[chunks][:],
                in1=gain[:, at].unsqueeze(2).to_broadcast([P, n, TOK]),
                op=ALU.mult,
            )

        def square(chunks):
            at = slice(chunks[0], chunks[0] + len(chunks))
            nc.scalar.activation(out=squares[:, at, :], in_=ckv[chunks][:], func=ACT.Square)

        def add_over_partitions(values, start=False, stop=False):
            nc.tensor.matmul(out=sum_sq[:], lhsT=ones[:], rhs=values, start=start, stop=stop)

        def keep_tensor_busy_mx(out, times):
            n = out.shape[1]
            rhs, rhs_scale = (wb_codes, wb_scales) if n > 2 * TOK else (x_codes, x_scales)
            if n <= 2 * TOK:
                rhs = rhs[:].rearrange("p g r -> p (g r)")
                rhs_scale = rhs_scale[:].rearrange("p g r -> p (g r)")
            for i in range(times):
                nc.tensor.matmul_mx(
                    out=out,
                    lhsT=x_codes[:, 0, :].bitcast(FP8X4),
                    lhsT_scale=x_scales[:, 0, :],
                    rhs=rhs[:, 0:n].bitcast(FP8X4),
                    rhs_scale=rhs_scale[:, 0:n],
                    start=True,
                    stop=True,
                )

        def second_product(parts):
            cols = slice(PART_ROWS * parts[0], PART_ROWS * (parts[-1] + 1))
            kv_ps = products.tile([P, PART_ROWS * len(parts)], F32, tag="product")
            if parts[0] < 4:
                keep_tensor_busy_mx(kv_ps[:], 1)
            nc.tensor.matmul_mx(
                out=kv_ps[:],
                lhsT=cn_codes[:].bitcast(FP8X4),
                lhsT_scale=cn_scales[:],
                rhs=wb_codes[:, cols].bitcast(FP8X4),
                rhs_scale=wb_scales[:, cols],
                start=True,
                stop=True,
            )
            banks["kv", parts] = kv_ps

        def copy_kv(copy_out, parts):
            group = [g for g in groups if parts[0] in g][0]
            lo = PART_ROWS * (parts[0] - group[0])
            copy_out(
                out=kv_sb[group][:, lo : lo + PART_ROWS * len(parts)].rearrange(
                    "p (h n i) -> p h n i", n=P, i=2
                ),
                in_=banks["kv", parts][:].rearrange("p (h i n) -> p h n i", n=P, i=2),
            )

        def store_kv(group, queues):
            heads = slice(2 * group[0], 2 * group[-1] + 2)
            for b in range(BATCH):
                by_head = kv_sb[group][b:P:BATCH, :].rearrange("s (h c) -> s h c", c=HEAD_COLS)
                queues[b].dma_start(
                    out=key_s[b, heads, :, 0:HALF_HEAD].rearrange("h s d -> s h d"),
                    in_=by_head[:, :, 0:HALF_HEAD],
                )
                queues[b].dma_start(
                    out=v[b, heads].rearrange("h s d -> s h d"), in_=by_head[:, :, HALF_HEAD:HEAD_COLS]
                )

        on_vector, on_scalar = nc.vector.tensor_copy, nc.scalar.copy

        for g, copy_out in ((0, on_vector), (1, on_scalar)):
            x_bank = staging.tile([P, 2, TOK], F32, tag="bank")
            transpose_words(nc, x_bank[:], x_sb[:, KR * g : KR * (g + 1)], ident[:])
            copy_out(
                out=x_grouped[:, g].bitcast(F32).rearrange("p (s b) u -> p s b u", b=BATCH),
                in_=x_bank[:].rearrange("p u (b s) -> p s b u", b=BATCH),
            )
        keep_tensor_busy(1)
        transpose_wa(0)
        regroup_wa(on_vector, 0)
        keep_tensor_busy(1)
        transpose_wa(1)
        regroup_wa(on_scalar, 1)
        nc.vector.quantize_mx(
            out=x_codes[:].rearrange("p g r -> p (g r)").bitcast(FP8X4),
            scales=x_scales[:].rearrange("p g r -> p (g r)"),
            in_=x_grouped[:].rearrange("p g r k -> p (g r k)"),
        )
        quantise_wa(0)
        transpose_wa(2)
        regroup_wa(on_scalar, 2)
        quantise_wa(1)
        transpose_wa(3, (0,))
        regroup_wa(on_vector, 3, (0,))
        transpose_wa(3, (1,))
        regroup_wa(on_scalar, 3, (1,))
        keep_tensor_busy_mx(ckv_01[:].rearrange("p c r -> p (c r)"), 2)
        quantise_wa(2)
        first_product(0)
        first_product(1)
        transpose_wb(0)
        quantise_wa(3)
        square((0, 1))
        first_product(2)
        first_product(3)
        multiply_by_gain((0, 1))
        regroup_wb(on_vector, 0)
        squares_01 = keep.tile([P, TOK], F32)
        nc.vector.tensor_tensor(out=squares_01[:], in0=squares[:, 0, :], in1=squares[:, 1, :], op=ALU.add)
        square((2,))
        square((3,))
        transpose_wb(1)
        add_over_partitions(squares[:, 2, :], start=True)
        add_over_partitions(squares[:, 3, :])
        add_over_partitions(squares_01[:], stop=True)
        multiply_by_gain((2,))
        multiply_by_gain((3,))
        quantise_wb(0)
        regroup_wb(on_scalar, 1)
        rstd = keep.tile([P, TOK], F32)
        nc.scalar.activation(
            out=rstd[:], in_=sum_sq[:], func=ACT.Abs_reciprocal_sqrt, bias=eps[:, 0:1], scale=1.0 / KR
        )
        transpose_wb(2)
        regroup_wb(on_scalar, 2)
        quantise_wb(1)
        cn_grouped = keep.tile([P, TOK, PACK], BF16, align_bytes=64)
        nc.vector.tensor_tensor(
            out=cn_grouped[:],
            in0=gained[:].rearrange("p t r -> p r t"),
            in1=rstd[:].unsqueeze(2).to_broadcast([P, TOK, PACK]),
            op=ALU.mult,
        )
        cn_codes = keep.tile([P, TOK], U32, align_bytes=64)
        cn_scales = keep.tile([P, TOK], U8, align_bytes=64)
        nc.vector.quantize_mx(
            out=cn_codes[:].bitcast(FP8X4),
            scales=cn_scales[:],
            in_=cn_grouped[:].rearrange("p r k -> p (r k)"),
        )
        transpose_wb(3)
        regroup_wb(on_scalar, 3)
        quantise_wb(2)
        transpose_wb(4)
        regroup_wb(on_vector, 4)
        quantise_wb(3)
        second_product((0, 1))
        copy_kv(on_scalar, (0, 1))
        store_kv(groups[0], (nc.sync, nc.sync))
        transpose_wb(5)
        regroup_wb(on_scalar, 5)
        quantise_wb(4)
        second_product((2, 3))
        copy_kv(on_scalar, (2, 3))
        store_kv(groups[1], (nc.sync, nc.sync))
        transpose_wb(6)
        quantise_wb(5)
        regroup_wb(on_vector, 6)
        transpose_wb(7)
        regroup_wb(on_scalar, 7)
        quantise_wb(6)
        second_product((4, 5))
        copy_kv(on_scalar, (4, 5))
        store_kv(groups[2], (nc.sync, nc.sync))
        quantise_wb(7)
        second_product((6,))
        second_product((7,))
        copy_kv(on_vector, (6,))
        copy_kv(on_scalar, (7,))
        store_kv(groups[3], (nc.sync, nc.sync))
